import numpy as np
import ml_dtypes


def mxq(x, axis, fmt="e4m3"):
    dtype, down = {"e4m3": (ml_dtypes.float8_e4m3fn, 7), "e5m2": (ml_dtypes.float8_e5m2, 14)}[fmt]
    v = np.moveaxis(np.asarray(x, np.float32).astype(ml_dtypes.bfloat16).astype(np.float64), axis, -1)
    blocks = v.reshape(v.shape[:-1] + (-1, 32))
    amax = np.abs(blocks).max(-1, keepdims=True)
    byte = np.maximum(np.where(amax > 0, np.frexp(amax)[1] - 1 + 127, 0) - down, 1)
    scale = np.exp2(byte - 127.0)
    codes = (blocks / scale).astype(np.float32).astype(dtype).astype(np.float64)
    return np.moveaxis((codes * scale).reshape(v.shape), -1, axis)


WIDE = False


def mx_kscale(k):
    if not WIDE:
        return np.ones(k)
    levels = np.array([30, -30])
    if k % 512:
        return np.exp2(np.random.permutation(np.resize(levels, k // 32))).repeat(32)
    a = np.empty((k // 512, 16))
    for p in range(k // 512):
        a[p, :8] = np.random.permutation(np.resize(levels, 8))
        for g in range(8):
            far = levels[np.abs(levels - a[p, g]) >= 10]
            a[p, g + 8] = far[np.random.randint(len(far))]
    return np.exp2(a.ravel()).repeat(32)


BF16 = ml_dtypes.bfloat16


def bf(x):
    return np.asarray(x, np.float32).astype(BF16)


def f64(x):
    return np.asarray(x).astype(np.float64)


B, S, D, H, KV, DH, QB = 1, 1024, 1024, 16, 4, 128, 512
HALF = DH // 2
EPS = 1e-6


def rope_tables():
    inv_freq = 1.0 / (10000.0 ** (np.arange(HALF) / HALF))
    ang = np.arange(S)[:, None] * inv_freq[None, :]
    ang = np.concatenate([ang, ang], axis=-1)
    return np.sin(ang), np.cos(ang)


def rmsnorm(u, scale, shift):
    rms = np.sqrt(np.mean(u * u, axis=-1, keepdims=True) + EPS)
    return u / rms * (1.0 + scale) + shift


def apply_rope(u, sin, cos):
    rot = np.concatenate([-u[..., HALF:], u[..., :HALF]], axis=-1)
    return u * cos[None, None, :S, :] + rot * sin[None, None, :S, :]


def heads(u, n):
    return u.reshape(B, S, n, DH).transpose(0, 2, 1, 3)


def setup_inputs():
    s = mx_kscale(D)
    sin, cos = rope_tables()
    return {"x": bf(np.random.standard_normal((B, S, D)) * s),
            "sin_thetas": bf(sin), "cos_thetas": bf(cos),
            "wq": bf(np.random.standard_normal((H * DH, D)) / np.sqrt(D) / s),
            "wk": bf(np.random.standard_normal((KV * DH, D)) / np.sqrt(D) / s),
            "wv": bf(np.random.standard_normal((KV * DH, D)) * 2.0 / np.sqrt(D) / s),
            "q_scale": bf(np.random.standard_normal(DH) * 0.1), "q_shift": bf(np.random.standard_normal(DH) * 0.1),
            "k_scale": bf(np.random.standard_normal(DH) * 0.1), "k_shift": bf(np.random.standard_normal(DH) * 0.1)}


def reference(x, sin_thetas, cos_thetas, wq, wk, wv, q_scale, q_shift, k_scale, k_shift):
    xq = mxq(f64(x), 2, "e5m2")
    q = heads(xq @ mxq(f64(wq), 1, "e5m2").T, H)
    k = heads(xq @ mxq(f64(wk), 1, "e5m2").T, KV)
    v = heads(xq @ mxq(f64(wv), 1, "e5m2").T, KV)
    q = rmsnorm(q, f64(q_scale), f64(q_shift))
    k = rmsnorm(k, f64(k_scale), f64(k_shift))
    q = apply_rope(q, f64(sin_thetas), f64(cos_thetas))
    k = apply_rope(k, f64(sin_thetas), f64(cos_thetas))
    return q, k, v

@@ -1,0 +1,309 @@
+from contextlib import ExitStack
+
+import concourse.mybir as mybir
+from concourse.masks import make_identity
+
+F32 = mybir.dt.float32
+BF16 = mybir.dt.bfloat16
+U32 = mybir.dt.uint32
+U8 = mybir.dt.uint8
+E5X4 = mybir.dt.float8_e5m2_x4
+ACT = mybir.ActivationFunctionType
+ALU = mybir.AluOpType
+
+P = 128
+SEQ = 1024
+KDIM = 1024
+DH = 128
+HALF = 64
+MT = SEQ // P
+EPS = 1e-6
+FLOPS = 2 * SEQ * KDIM * 3072
+OFFLOAD_EVERY = 4
+
+
+def tile_groupqueryattention_pa_kernel(
+    tc, x, sin_thetas, cos_thetas, wq, wk, wv, q_scale, q_shift, k_scale, k_shift, out_0, out_1, out_2
+):
+    nc = tc.nc
+    with ExitStack() as ctx:
+        const = ctx.enter_context(tc.tile_pool(name="const", bufs=1))
+        work = ctx.enter_context(tc.tile_pool(name="work", bufs=1))
+        psum = ctx.enter_context(tc.psum_pool(name="psum", bufs=1))
+
+        vec_rows = const.tile([P, 4 * DH], BF16, name="vec_rows")
+        nc.gpsimd.memset(vec_rows[:], 0.0)
+        for j, vec in enumerate((q_scale, q_shift, k_scale, k_shift)):
+            nc.sync.dma_start(
+                out=vec_rows[0:1, j * DH : (j + 1) * DH], in_=vec.rearrange("(o d) -> o d", o=1)
+            )
+        cos_sb = const.tile([P, MT, DH], BF16, name="cos_sb")
+        sin_sb = const.tile([P, MT, DH], BF16, name="sin_sb")
+
+        x_view = x[0].rearrange("(p m) k -> p m k", m=MT)
+        x_sb = []
+        w_sb = {}
+
+        def load_x(pair):
+            t = const.tile([P, 2, KDIM], BF16, name="x_sb%d" % pair)
+            nc.sync.dma_start(out=t[:], in_=x_view[:, 2 * pair : 2 * pair + 2, :])
+            x_sb.append(t)
+
+        def load_w(key, w, row0):
+            halves = []
+            for hf in range(2):
+                t = const.tile([P, 2, KDIM], BF16, name="w_sb_%s_%d" % (key, hf))
+                nc.sync.dma_start(
+                    out=t[:],
+                    in_=w[row0 + 256 * hf : row0 + 256 * (hf + 1), :].rearrange("(c p) k -> p c k", p=P),
+                )
+                halves.append(t)
+            w_sb[key] = halves
+
+        load_x(0)
+        load_w("q0", wq, 0)
+        nc.sync.dma_start(out=cos_sb[:], in_=cos_thetas.rearrange("(p m) d -> p m d", m=MT))
+        nc.sync.dma_start(out=sin_sb[:], in_=sin_thetas.rearrange("(p m) d -> p m d", m=MT))
+        load_x(1)
+        load_x(2)
+        load_x(3)
+        load_w("v", wv, 0)
+        load_w("q1", wq, 512)
+        load_w("q2", wq, 1024)
+        load_w("q3", wq, 1536)
+        load_w("k", wk, 0)
+
+        ident = const.tile([P, P], F32, name="ident")
+        make_identity(nc, ident[:])
+        ident_bf = const.tile([P, P], BF16, name="ident_bf")
+        make_identity(nc, ident_bf[:])
+        ones = const.tile([P, P], BF16, name="ones")
+        nc.vector.memset(ones[:], 1.0)
+        warm = const.tile([P, 1], F32, name="warm")
+        nc.vector.memset(warm[:], 1.0)
+        nc.scalar.activation(out=warm[:], in_=warm[:], func=ACT.Abs_reciprocal_sqrt)
+
+        bc_ps = psum.tile([P, 512], F32, tag="tp", bufs=2, name="bc_ps")
+        nc.tensor.matmul(out=bc_ps[:], lhsT=ones[:], rhs=vec_rows[:], start=True, stop=True)
+        bc4 = bc_ps[:].rearrange("p (t s d) -> p t s d", t=2, s=2)
+        gain4 = const.tile([P, 2, 4 * HALF], F32, name="gain4")
+        vec2 = const.tile([P, 2, 2, 4 * HALF], F32, name="vec2")
+        nc.vector.tensor_scalar_add(out=gain4[:, :, 0:64], in0=bc4[:, :, 0, 0:64], scalar1=1.0)
+        nc.vector.tensor_scalar(
+            out=gain4[:, :, 64:128], in0=bc4[:, :, 0, 64:128], scalar1=-1.0, scalar2=-1.0,
+            op0=ALU.mult, op1=ALU.add,
+        )
+        nc.vector.tensor_scalar_add(out=gain4[:, :, 128:256], in0=bc4[:, :, 0, :], scalar1=1.0)
+        nc.vector.tensor_copy(out=vec2[:, :, :, 0:128], in_=bc4[:, :, :, :])
+        nc.vector.tensor_scalar_mul(out=vec2[:, :, :, 128:192], in0=bc4[:, :, :, 64:128], scalar1=-1.0)
+        nc.vector.tensor_copy(out=vec2[:, :, :, 192:256], in_=bc4[:, :, :, 0:64])
+        dmat = const.tile([P, 8, DH], BF16, name="dmat")
+        nc.vector.tensor_tensor(
+            out=dmat[:], in0=ident[:].unsqueeze(1).to_broadcast([P, 8, DH]),
+            in1=vec2[:].rearrange("p t s (j d) -> p (t s j) d", j=2), op=ALU.mult,
+        )
+        unit2 = const.tile([P, 2, DH], BF16, name="unit2")
+        nc.vector.tensor_copy(out=unit2[:, 0, :], in_=ident_bf[:])
+        nc.vector.tensor_scalar_mul(out=unit2[:, 1, 0:64], in0=ident_bf[:, 0:64], scalar1=-1.0)
+        nc.vector.tensor_copy(out=unit2[:, 1, 64:128], in_=ident_bf[:, 64:128])
+
+        def over_m(ap, n_m):
+            return ap.unsqueeze(1).to_broadcast([P, n_m, ap.shape[1]])
+
+        def tab_steps(eng, tab, t, m0, m1):
+            ms = slice(m0, m1)
+            return [
+                lambda: eng.tensor_tensor(out=tab[:, ms, 0:64], in0=cos_sb[:, ms, 0:64],
+                                          in1=over_m(gain4[:, t, 0:64], m1 - m0), op=ALU.mult),
+                lambda: eng.tensor_tensor(out=tab[:, ms, 64:192], in0=sin_sb[:, ms, :],
+                                          in1=over_m(gain4[:, t, 64:192], m1 - m0), op=ALU.mult),
+                lambda: eng.tensor_tensor(out=tab[:, ms, 192:256], in0=cos_sb[:, ms, 64:128],
+                                          in1=over_m(gain4[:, t, 192:256], m1 - m0), op=ALU.mult),
+            ]
+
+        def trig_transposed():
+            trig_t = const.tile([P, 2, MT, P], BF16, name="trig_t")
+            for j, src in enumerate((cos_sb, sin_sb)):
+                tps = psum.tile([P, MT, P], BF16, tag="acc", bufs=4, name="tps")
+                for m in range(MT):
+                    nc.tensor.transpose(tps[:, m, :], src[:, m, :], ident_bf[:])
+                nc.scalar.copy(out=trig_t[:, j, :, :], in_=tps[:])
+            return trig_t
+
+        def c_tables(trig_t, t, c_sb):
+            banks = []
+            for j in range(2):
+                cps = psum.tile([P, 4, DH], F32, tag="cps", bufs=2, name="cps")
+                for i in range(4):
+                    nc.tensor.matmul(out=cps[:, i, :], lhsT=trig_t[:, 0, 4 * j + i, :], rhs=dmat[:, 4 * t + 2, :],
+                                     start=True, stop=False)
+                    nc.tensor.matmul(out=cps[:, i, :], lhsT=trig_t[:, 1, 4 * j + i, :], rhs=dmat[:, 4 * t + 3, :],
+                                     start=False, stop=True)
+                nc.scalar.copy(out=c_sb[:, 4 * j : 4 * j + 4, :], in_=cps[:])
+                banks.append(cps)
+            return banks
+
+        def tab_k_pair(trig_t, m0):
+            tps = psum.tile([P, 2, 4 * HALF], F32, tag="tp", bufs=2, name="tabps")
+            for i in range(2):
+                out4 = tps[:, i, :].rearrange("p (k e) -> p k e", k=4)
+                for j, out_j in ((0, out4[:, 0:4:3, :]), (1, out4[:, 1:3, :])):
+                    nc.tensor.matmul(out=out_j, lhsT=trig_t[:, j, m0 + i, :],
+                                     rhs=unit2[:, j, :].rearrange("p (k e) -> p k e", k=2), start=True, stop=False)
+                    nc.tensor.matmul(out=out_j, lhsT=trig_t[:, j, m0 + i, :],
+                                     rhs=dmat[:, 4 + j, :].rearrange("p (k e) -> p k e", k=2), start=False, stop=True)
+            nc.scalar.copy(out=tab_k[:, m0 : m0 + 2, :], in_=tps[:])
+
+        tab_q = const.tile([P, MT, 4 * HALF], F32, name="tab_q")
+        tab_k = const.tile([P, MT, 4 * HALF], F32, name="tab_k")
+        c_q = const.tile([P, MT, DH], F32, name="c_q")
+        c_k = const.tile([P, MT, DH], F32, name="c_k")
+        for step in tab_steps(nc.gpsimd, tab_q, 0, 0, 2) + tab_steps(nc.gpsimd, tab_q, 0, 2, MT):
+            step()
+
+        def prep(name, srcs, widths, share=False):
+            rows = 256 * len(srcs)
+            grouped = work.tile([P, 8 * rows], BF16, tag="grouped", bufs=3, name="grouped", align_bytes=64)
+            gw = grouped[:].bitcast(F32)
+            codes = const.tile([P, 2 * rows], U32, name="codes_" + name, align_bytes=64)
+            scales = const.tile([P, 2 * rows], U8, name="scales_" + name, align_bytes=64)
+            for s, src in enumerate(srcs):
+                for g in range(2):
+                    tp = psum.tile([P, 2, 256], F32, tag="tp", bufs=2, name="tp")
+                    for c in range(2):
+                        words = src[:, c, :].bitcast(F32)
+                        for u in range(2):
+                            nc.tensor.transpose(
+                                tp[:, u, c * P : (c + 1) * P],
+                                words[:, 256 * g + u : 256 * (g + 1) : 2],
+                                ident[:],
+                            )
+                    w0 = (g * rows + s * 256) * 2
+                    if share and g == 1:
+                        nc.vector.tensor_copy(
+                            out=gw[:, w0 : w0 + 512].rearrange("p (r u) -> p r u", u=2),
+                            in_=tp[:].rearrange("p u r -> p r u"),
+                        )
+                    else:
+                        nc.scalar.copy(
+                            out=gw[:, w0 : w0 + 512].rearrange("p (r u) -> p r u", u=2),
+                            in_=tp[:].rearrange("p u r -> p r u"),
+                        )
+            for c0 in range(0, 2 * rows, widths):
+                nc.vector.quantize_mx(
+                    out=codes[:, c0 : c0 + widths].bitcast(E5X4),
+                    scales=scales[:, c0 : c0 + widths],
+                    in_=grouped[:, 4 * c0 : 4 * (c0 + widths)],
+                )
+            return codes, scales
+
+        xq = {}
+        wqz = {}
+
+        def prep_x(pair, widths=512, share=False):
+            xq[pair] = prep("x%d" % pair, [x_sb[pair]], widths, share)
+
+        def prep_w(key, widths=1024, share=False):
+            wqz[key] = prep("w" + key, w_sb[key], widths, share)
+
+        def mx_bank(m, key):
+            acc = psum.tile([P, 512], F32, tag="acc", bufs=4, name="acc")
+            pair, half = divmod(m, 2)
+            xc, xs = xq[pair]
+            wc, ws = wqz[key]
+            for g in range(2):
+                xcols = slice(g * 256 + half * P, g * 256 + (half + 1) * P)
+                wcols = slice(g * 512, (g + 1) * 512)
+                nc.tensor.matmul_mx(
+                    out=acc[:],
+                    lhsT=xc[:, xcols].bitcast(E5X4), lhsT_scale=xs[:, xcols],
+                    rhs=wc[:, wcols].bitcast(E5X4), rhs_scale=ws[:, wcols],
+                    start=(g == 0), stop=(g == 1),
+                )
+            return acc
+
+        def out_view(out, h0):
+            return out[0, h0 : h0 + 4, :, :].rearrange("h (p m) d -> p h m d", m=MT)
+
+        state = {"late": 0}
+
+        def normed_bank(m, key, tab, cps, c_sb, out, h0, group, offload):
+            acc = mx_bank(m, key)
+            prod = work.tile([P, 4, 4 * HALF], F32, tag="prod", bufs=6, name="prod")
+            nc.vector.tensor_tensor(
+                out=prod[:].rearrange("p h (k d) -> p h k d", k=2),
+                in0=tab[:, m, :].rearrange("p (k d) -> p k d", k=2).unsqueeze(1).to_broadcast([P, 4, 2, DH]),
+                in1=acc[:].rearrange("p (h d) -> p h d", h=4).unsqueeze(2).to_broadcast([P, 4, 2, DH]),
+                op=ALU.mult,
+            )
+            ss = work.tile([P, 4], F32, tag="ss", bufs=6, name="ss")
+            junk = work.tile([P, DH], F32, tag="junk", bufs=2, name="junk")
+            for h in range(4):
+                nc.scalar.activation(out=junk[:], in_=acc[:, h * DH : (h + 1) * DH], func=ACT.Square,
+                                     accum_out=ss[:, h : h + 1])
+            rinv = work.tile([P, 4], F32, tag="rinv", bufs=6, name="rinv")
+            nc.scalar.activation(out=rinv[:], in_=ss[:], func=ACT.Abs_reciprocal_sqrt, bias=EPS, scale=1.0 / DH)
+            prod4 = prod[:].rearrange("p h (k e) -> p h k e", k=4)
+            rot = work.tile([P, 4, DH], F32, tag="rot", bufs=6, name="rot")
+            nc.gpsimd.tensor_tensor(
+                out=rot[:].rearrange("p h (t e) -> p h t e", t=2),
+                in0=prod4[:, :, 0:4:3, :], in1=prod4[:, :, 1:3, :], op=ALU.add,
+            )
+            mm = m % group
+            if mm == 0:
+                state["o"] = work.tile([P, 4, group, DH], F32, tag="o", bufs=4, name="o")
+            o = state["o"]
+            if offload:
+                scaled = work.tile([P, 4, DH], F32, tag="scaled", bufs=3, name="scaled")
+                for h in range(4):
+                    nc.scalar.activation(out=scaled[:, h, :], in_=rot[:, h, :], func=ACT.Copy,
+                                         scale=rinv[:, h : h + 1])
+                nc.gpsimd.tensor_tensor(out=o[:, :, mm, :], in0=scaled[:],
+                                        in1=c_sb[:, m, :].unsqueeze(1).to_broadcast([P, 4, DH]), op=ALU.add)
+            else:
+                for h in range(4):
+                    nc.vector.scalar_tensor_tensor(
+                        out=o[:, h, mm, :], in0=rot[:, h, :], scalar=rinv[:, h : h + 1],
+                        in1=cps[m // 4][:, m % 4, :], op0=ALU.mult, op1=ALU.add,
+                    )
+            if mm == group - 1:
+                nc.sync.dma_start(out=out_view(out, h0)[:, :, m - mm : m + 1, :], in_=o[:])
+
+        def plain_bank(m):
+            acc = mx_bank(m, "v")
+            mm = m % 2
+            if mm == 0:
+                state["ov"] = work.tile([P, 4, 2, DH], F32, tag="ov", bufs=2, name="ov")
+            ov = state["ov"]
+            nc.scalar.copy(out=ov[:, :, mm, :], in_=acc[:].rearrange("p (h d) -> p h d", h=4))
+            if mm == 1:
+                nc.sync.dma_start(out=out_view(out_2, 0)[:, :, m - 1 : m + 1, :], in_=ov[:])
+
+        prep_x(0, 256, True)
+        prep_w("q0", 256, True)
+        prep_x(1)
+        trig_t = trig_transposed()
+        cps_q = c_tables(trig_t, 0, c_q)
+        main = ["q0", "q1", "q2", "q3", "k"]
+        extra = {(0, 1): lambda: prep_x(2), (0, 3): lambda: prep_x(3), (0, 4): lambda: prep_w("q1"),
+                 (0, 6): lambda: prep_w("v")}
+        cps_now = cps_q
+        for ci, key in enumerate(main):
+            if key == "k":
+                cps_now = c_tables(trig_t, 1, c_k)
+            for m in range(MT):
+                b = MT * ci + m
+                offload = b % OFFLOAD_EVERY == OFFLOAD_EVERY - 1 and b < 37
+                if key == "k":
+                    normed_bank(m, key, tab_k, cps_now, c_k, out_1, 0, 2 if m < 6 else 1, offload)
+                else:
+                    normed_bank(m, key, tab_q, cps_now, c_q, out_0, 4 * ci, 2, offload)
+                if (ci, m) in extra:
+                    extra[(ci, m)]()
+                if ci >= 1 and m == 2 and ci + 1 < len(main):
+                    prep_w(main[ci + 1])
+                if ci >= 1 and m in (1, 5):
+                    plain_bank(2 * (ci - 1) + (m - 1) // 4)
+                if ci in (1, 2) and m in (3, 7):
+                    tab_k_pair(trig_t, state["late"])
+                    state["late"] = state["late"] + 2

@@ -83,7 +83,7 @@ def tile_groupqueryattention_pa_kernel(
         nc.vector.memset(warm[:], 1.0)
         nc.scalar.activation(out=warm[:], in_=warm[:], func=ACT.Abs_reciprocal_sqrt)
 
-        bc_ps = psum.tile([P, 512], F32, tag="tp", bufs=2, name="bc_ps")
+        bc_ps = psum.tile([P, 512], F32, tag="bank", bufs=6, name="bc_ps")
         nc.tensor.matmul(out=bc_ps[:], lhsT=ones[:], rhs=vec_rows[:], start=True, stop=True)
         bc4 = bc_ps[:].rearrange("p (t s d) -> p t s d", t=2, s=2)
         gain4 = const.tile([P, 2, 4 * HALF], F32, name="gain4")
@@ -124,7 +124,7 @@ def tile_groupqueryattention_pa_kernel(
         def trig_transposed():
             trig_t = const.tile([P, 2, MT, P], BF16, name="trig_t")
             for j, src in enumerate((cos_sb, sin_sb)):
-                tps = psum.tile([P, MT, P], BF16, tag="acc", bufs=4, name="tps")
+                tps = psum.tile([P, MT, P], BF16, tag="bank", bufs=6, name="tps")
                 for m in range(MT):
                     nc.tensor.transpose(tps[:, m, :], src[:, m, :], ident_bf[:])
                 nc.scalar.copy(out=trig_t[:, j, :, :], in_=tps[:])
@@ -144,7 +144,7 @@ def tile_groupqueryattention_pa_kernel(
             return banks
 
         def tab_k_pair(trig_t, m0):
-            tps = psum.tile([P, 2, 4 * HALF], F32, tag="tp", bufs=2, name="tabps")
+            tps = psum.tile([P, 2, 4 * HALF], F32, tag="bank", bufs=6, name="tabps")
             for i in range(2):
                 out4 = tps[:, i, :].rearrange("p (k e) -> p k e", k=4)
                 for j, out_j in ((0, out4[:, 0:4:3, :]), (1, out4[:, 1:3, :])):
@@ -169,7 +169,7 @@ def tile_groupqueryattention_pa_kernel(
             scales = const.tile([P, 2 * rows], U8, name="scales_" + name, align_bytes=64)
             for s, src in enumerate(srcs):
                 for g in range(2):
-                    tp = psum.tile([P, 2, 256], F32, tag="tp", bufs=2, name="tp")
+                    tp = psum.tile([P, 2, 256], F32, tag="bank", bufs=6, name="tp")
                     for c in range(2):
                         words = src[:, c, :].bitcast(F32)
                         for u in range(2):
@@ -207,7 +207,7 @@ def tile_groupqueryattention_pa_kernel(
             wqz[key] = prep("w" + key, w_sb[key], widths, share)
 
         def mx_bank(m, key):
-            acc = psum.tile([P, 512], F32, tag="acc", bufs=4, name="acc")
+            acc = psum.tile([P, 512], F32, tag="bank", bufs=6, name="acc")
             pair, half = divmod(m, 2)
             xc, xs = xq[pair]
             wc, ws = wqz[key]

@@ -19,7 +19,15 @@ HALF = 64
 MT = SEQ // P
 EPS = 1e-6
 FLOPS = 2 * SEQ * KDIM * 3072
-OFFLOAD_EVERY = 4
+AHEAD = 2
+LAG_V = 2
+LAG_S = 2
+LAG_G = 3
+P_SET = range(0, 0, 3)
+O_SET = range(1, 37, 4)
+V0 = 17
+VSTEP = 2
+QLAG = 6
 
 
 def tile_groupqueryattention_pa_kernel(
@@ -32,22 +40,32 @@ def tile_groupqueryattention_pa_kernel(
         psum = ctx.enter_context(tc.psum_pool(name="psum", bufs=1))
 
         vec_rows = const.tile([P, 4 * DH], BF16, name="vec_rows")
-        nc.gpsimd.memset(vec_rows[:], 0.0)
-        for j, vec in enumerate((q_scale, q_shift, k_scale, k_shift)):
-            nc.sync.dma_start(
-                out=vec_rows[0:1, j * DH : (j + 1) * DH], in_=vec.rearrange("(o d) -> o d", o=1)
-            )
+        nc.vector.memset(vec_rows[:], 0.0)
         cos_sb = const.tile([P, MT, DH], BF16, name="cos_sb")
         sin_sb = const.tile([P, MT, DH], BF16, name="sin_sb")
 
         x_view = x[0].rearrange("(p m) k -> p m k", m=MT)
-        x_sb = []
+        x_sb = {}
+        x_first = []
+        w_first = []
         w_sb = {}
 
         def load_x(pair):
             t = const.tile([P, 2, KDIM], BF16, name="x_sb%d" % pair)
             nc.sync.dma_start(out=t[:], in_=x_view[:, 2 * pair : 2 * pair + 2, :])
-            x_sb.append(t)
+            x_sb[pair] = t
+
+        def load_x_tile(m):
+            t = const.tile([P, KDIM], BF16, name="x_first%d" % m)
+            nc.sync.dma_start(out=t[:], in_=x_view[:, m, :])
+            x_first.append(t)
+
+        def load_w_by_k(key, w, row0, g):
+            t = const.tile([P, 4, 512], BF16, name="w_sb_%s_k%d" % (key, g))
+            nc.sync.dma_start(
+                out=t[:], in_=w[row0 : row0 + 512, 512 * g : 512 * (g + 1)].rearrange("(c p) k -> p c k", p=P)
+            )
+            w_first.append(t)
 
         def load_w(key, w, row0):
             halves = []
@@ -60,18 +78,25 @@ def tile_groupqueryattention_pa_kernel(
                 halves.append(t)
             w_sb[key] = halves
 
-        load_x(0)
-        load_w("q0", wq, 0)
-        nc.sync.dma_start(out=cos_sb[:], in_=cos_thetas.rearrange("(p m) d -> p m d", m=MT))
-        nc.sync.dma_start(out=sin_sb[:], in_=sin_thetas.rearrange("(p m) d -> p m d", m=MT))
-        load_x(1)
-        load_x(2)
-        load_x(3)
-        load_w("v", wv, 0)
-        load_w("q1", wq, 512)
-        load_w("q2", wq, 1024)
-        load_w("q3", wq, 1536)
-        load_w("k", wk, 0)
+        with tc.manual_schedule(engines={mybir.EngineType.SP}):
+            load_x_tile(0)
+            load_w_by_k("q0", wq, 0, 0)
+            for j, vec in enumerate((q_scale, q_shift, k_scale, k_shift)):
+                nc.sync.dma_start(
+                    out=vec_rows[0:1, j * DH : (j + 1) * DH], in_=vec.rearrange("(o d) -> o d", o=1)
+                )
+            load_w_by_k("q0", wq, 0, 1)
+            nc.sync.dma_start(out=cos_sb[:], in_=cos_thetas.rearrange("(p m) d -> p m d", m=MT))
+            nc.sync.dma_start(out=sin_sb[:], in_=sin_thetas.rearrange("(p m) d -> p m d", m=MT))
+            load_x_tile(1)
+            load_x(1)
+            load_x(2)
+            load_x(3)
+            load_w("q1", wq, 512)
+            load_w("v", wv, 0)
+            load_w("q2", wq, 1024)
+            load_w("q3", wq, 1536)
+            load_w("k", wk, 0)
 
         ident = const.tile([P, P], F32, name="ident")
         make_identity(nc, ident[:])
@@ -83,29 +108,35 @@ def tile_groupqueryattention_pa_kernel(
         nc.vector.memset(warm[:], 1.0)
         nc.scalar.activation(out=warm[:], in_=warm[:], func=ACT.Abs_reciprocal_sqrt)
 
-        bc_ps = psum.tile([P, 512], F32, tag="bank", bufs=6, name="bc_ps")
-        nc.tensor.matmul(out=bc_ps[:], lhsT=ones[:], rhs=vec_rows[:], start=True, stop=True)
-        bc4 = bc_ps[:].rearrange("p (t s d) -> p t s d", t=2, s=2)
         gain4 = const.tile([P, 2, 4 * HALF], F32, name="gain4")
         vec2 = const.tile([P, 2, 2, 4 * HALF], F32, name="vec2")
-        nc.vector.tensor_scalar_add(out=gain4[:, :, 0:64], in0=bc4[:, :, 0, 0:64], scalar1=1.0)
-        nc.vector.tensor_scalar(
-            out=gain4[:, :, 64:128], in0=bc4[:, :, 0, 64:128], scalar1=-1.0, scalar2=-1.0,
-            op0=ALU.mult, op1=ALU.add,
-        )
-        nc.vector.tensor_scalar_add(out=gain4[:, :, 128:256], in0=bc4[:, :, 0, :], scalar1=1.0)
-        nc.vector.tensor_copy(out=vec2[:, :, :, 0:128], in_=bc4[:, :, :, :])
-        nc.vector.tensor_scalar_mul(out=vec2[:, :, :, 128:192], in0=bc4[:, :, :, 64:128], scalar1=-1.0)
-        nc.vector.tensor_copy(out=vec2[:, :, :, 192:256], in_=bc4[:, :, :, 0:64])
         dmat = const.tile([P, 8, DH], BF16, name="dmat")
-        nc.vector.tensor_tensor(
-            out=dmat[:], in0=ident[:].unsqueeze(1).to_broadcast([P, 8, DH]),
-            in1=vec2[:].rearrange("p t s (j d) -> p (t s j) d", j=2), op=ALU.mult,
-        )
         unit2 = const.tile([P, 2, DH], BF16, name="unit2")
-        nc.vector.tensor_copy(out=unit2[:, 0, :], in_=ident_bf[:])
-        nc.vector.tensor_scalar_mul(out=unit2[:, 1, 0:64], in0=ident_bf[:, 0:64], scalar1=-1.0)
-        nc.vector.tensor_copy(out=unit2[:, 1, 64:128], in_=ident_bf[:, 64:128])
+
+        def spread_vectors():
+            bc_ps = psum.tile([P, 512], F32, tag="bank", bufs=6, name="bc_ps")
+            nc.tensor.matmul(out=bc_ps[:], lhsT=ones[:], rhs=vec_rows[:], start=True, stop=True)
+            return bc_ps[:].rearrange("p (t s d) -> p t s d", t=2, s=2)
+
+        def gains(bc4):
+            nc.vector.tensor_scalar_add(out=gain4[:, :, 0:64], in0=bc4[:, :, 0, 0:64], scalar1=1.0)
+            nc.vector.tensor_scalar(
+                out=gain4[:, :, 64:128], in0=bc4[:, :, 0, 64:128], scalar1=-1.0, scalar2=-1.0,
+                op0=ALU.mult, op1=ALU.add,
+            )
+            nc.vector.tensor_scalar_add(out=gain4[:, :, 128:256], in0=bc4[:, :, 0, :], scalar1=1.0)
+
+        def late_constants(bc4):
+            nc.vector.tensor_copy(out=vec2[:, :, :, 0:128], in_=bc4[:, :, :, :])
+            nc.vector.tensor_scalar_mul(out=vec2[:, :, :, 128:192], in0=bc4[:, :, :, 64:128], scalar1=-1.0)
+            nc.vector.tensor_copy(out=vec2[:, :, :, 192:256], in_=bc4[:, :, :, 0:64])
+            nc.vector.tensor_tensor(
+                out=dmat[:], in0=ident[:].unsqueeze(1).to_broadcast([P, 8, DH]),
+                in1=vec2[:].rearrange("p t s (j d) -> p (t s j) d", j=2), op=ALU.mult,
+            )
+            nc.vector.tensor_copy(out=unit2[:, 0, :], in_=ident_bf[:])
+            nc.vector.tensor_scalar_mul(out=unit2[:, 1, 0:64], in0=ident_bf[:, 0:64], scalar1=-1.0)
+            nc.vector.tensor_copy(out=unit2[:, 1, 64:128], in_=ident_bf[:, 64:128])
 
         def over_m(ap, n_m):
             return ap.unsqueeze(1).to_broadcast([P, n_m, ap.shape[1]])
@@ -130,7 +161,7 @@ def tile_groupqueryattention_pa_kernel(
                 nc.scalar.copy(out=trig_t[:, j, :, :], in_=tps[:])
             return trig_t
 
-        def c_tables(trig_t, t, c_sb):
+        def c_tables(trig_t, t):
             banks = []
             for j in range(2):
                 cps = psum.tile([P, 4, DH], F32, tag="cps", bufs=2, name="cps")
@@ -139,9 +170,11 @@ def tile_groupqueryattention_pa_kernel(
                                      start=True, stop=False)
                     nc.tensor.matmul(out=cps[:, i, :], lhsT=trig_t[:, 1, 4 * j + i, :], rhs=dmat[:, 4 * t + 3, :],
                                      start=False, stop=True)
-                nc.scalar.copy(out=c_sb[:, 4 * j : 4 * j + 4, :], in_=cps[:])
                 banks.append(cps)
             return banks
+
+        def c_copy(banks, c_sb, j):
+            nc.scalar.copy(out=c_sb[:, 4 * j : 4 * j + 4, :], in_=banks[j][:])
 
         def tab_k_pair(trig_t, m0):
             tps = psum.tile([P, 2, 4 * HALF], F32, tag="bank", bufs=6, name="tabps")
@@ -158,66 +191,71 @@ def tile_groupqueryattention_pa_kernel(
         tab_k = const.tile([P, MT, 4 * HALF], F32, name="tab_k")
         c_q = const.tile([P, MT, DH], F32, name="c_q")
         c_k = const.tile([P, MT, DH], F32, name="c_k")
-        for step in tab_steps(nc.gpsimd, tab_q, 0, 0, 2) + tab_steps(nc.gpsimd, tab_q, 0, 2, MT):
-            step()
 
-        def prep(name, srcs, widths, share=False):
+
+        operands = {}
+
+        def operand(name, srcs):
             rows = 256 * len(srcs)
-            grouped = work.tile([P, 8 * rows], BF16, tag="grouped", bufs=3, name="grouped", align_bytes=64)
-            gw = grouped[:].bitcast(F32)
-            codes = const.tile([P, 2 * rows], U32, name="codes_" + name, align_bytes=64)
-            scales = const.tile([P, 2 * rows], U8, name="scales_" + name, align_bytes=64)
-            for s, src in enumerate(srcs):
-                for g in range(2):
-                    tp = psum.tile([P, 2, 256], F32, tag="bank", bufs=6, name="tp")
-                    for c in range(2):
-                        words = src[:, c, :].bitcast(F32)
-                        for u in range(2):
-                            nc.tensor.transpose(
-                                tp[:, u, c * P : (c + 1) * P],
-                                words[:, 256 * g + u : 256 * (g + 1) : 2],
-                                ident[:],
-                            )
-                    w0 = (g * rows + s * 256) * 2
-                    if share and g == 1:
-                        nc.vector.tensor_copy(
-                            out=gw[:, w0 : w0 + 512].rearrange("p (r u) -> p r u", u=2),
-                            in_=tp[:].rearrange("p u r -> p r u"),
-                        )
-                    else:
-                        nc.scalar.copy(
-                            out=gw[:, w0 : w0 + 512].rearrange("p (r u) -> p r u", u=2),
-                            in_=tp[:].rearrange("p u r -> p r u"),
-                        )
-            for c0 in range(0, 2 * rows, widths):
-                nc.vector.quantize_mx(
-                    out=codes[:, c0 : c0 + widths].bitcast(E5X4),
-                    scales=scales[:, c0 : c0 + widths],
-                    in_=grouped[:, 4 * c0 : 4 * (c0 + widths)],
-                )
-            return codes, scales
+            operands[name] = {
+                "srcs": srcs,
+                "grouped": work.tile([P, 8 * rows], BF16, tag="grouped", bufs=3, name="grouped", align_bytes=64),
+                "codes": const.tile([P, 2 * rows], U32, name="codes_" + name, align_bytes=64),
+                "scales": const.tile([P, 2 * rows], U8, name="scales_" + name, align_bytes=64),
+                "banks": [],
+            }
 
-        xq = {}
-        wqz = {}
+        def turn(name, s, g, tag="tp"):
+            tp = psum.tile([P, 2, 256], F32, tag="bank", bufs=6, name="tp")
+            for c in range(2):
+                if name == "q0":
+                    words = w_first[g][:, 2 * s + c, :].bitcast(F32)
+                else:
+                    words = operands[name]["srcs"][s][:, c, 512 * g : 512 * (g + 1)].bitcast(F32)
+                for u in range(2):
+                    nc.tensor.transpose(tp[:, u, c * P : (c + 1) * P], words[:, u::2], ident[:])
+            operands[name]["banks"].append((s, g, tp))
 
-        def prep_x(pair, widths=512, share=False):
-            xq[pair] = prep("x%d" % pair, [x_sb[pair]], widths, share)
+        def turn_x_tile(m):
+            tp = psum.tile([P, 2, 2, P], F32, tag="bank", bufs=6, name="tp")
+            words = x_first[m][:].bitcast(F32)
+            for g in range(2):
+                for u in range(2):
+                    nc.tensor.transpose(tp[:, g, u, :], words[:, 256 * g + u : 256 * (g + 1) : 2], ident[:])
+            return tp
 
-        def prep_w(key, widths=1024, share=False):
-            wqz[key] = prep("w" + key, w_sb[key], widths, share)
+        def finish_x_tile(m, tp):
+            o = operands["x0"]
+            gw = o["grouped"][:].bitcast(F32).rearrange("p (g r u) -> p g r u", g=2, u=2)
+            nc.scalar.copy(out=gw[:, :, m * P : (m + 1) * P, :], in_=tp[:].rearrange("p g u r -> p g r u"))
+            for g in range(2):
+                c0 = 256 * g + m * P
+                quantise("x0", c0, c0 + P)
+
+        def copy_out(name, vector=False):
+            s, g, tp = operands[name]["banks"].pop(0)
+            rows = 256 * len(operands[name]["srcs"])
+            w0 = (g * rows + s * 256) * 2
+            gw = operands[name]["grouped"][:].bitcast(F32)
+            eng = nc.vector.tensor_copy if vector else nc.scalar.copy
+            eng(out=gw[:, w0 : w0 + 512].rearrange("p (r u) -> p r u", u=2), in_=tp[:].rearrange("p u r -> p r u"))
+
+        def quantise(name, c0, c1):
+            o = operands[name]
+            nc.vector.quantize_mx(out=o["codes"][:, c0:c1].bitcast(E5X4), scales=o["scales"][:, c0:c1],
+                                  in_=o["grouped"][:, 4 * c0 : 4 * c1])
 
         def mx_bank(m, key):
             acc = psum.tile([P, 512], F32, tag="bank", bufs=6, name="acc")
             pair, half = divmod(m, 2)
-            xc, xs = xq[pair]
-            wc, ws = wqz[key]
+            xo, wo = operands["x%d" % pair], operands[key]
             for g in range(2):
                 xcols = slice(g * 256 + half * P, g * 256 + (half + 1) * P)
                 wcols = slice(g * 512, (g + 1) * 512)
                 nc.tensor.matmul_mx(
                     out=acc[:],
-                    lhsT=xc[:, xcols].bitcast(E5X4), lhsT_scale=xs[:, xcols],
-                    rhs=wc[:, wcols].bitcast(E5X4), rhs_scale=ws[:, wcols],
+                    lhsT=xo["codes"][:, xcols].bitcast(E5X4), lhsT_scale=xo["scales"][:, xcols],
+                    rhs=wo["codes"][:, wcols].bitcast(E5X4), rhs_scale=wo["scales"][:, wcols],
                     start=(g == 0), stop=(g == 1),
                 )
             return acc
@@ -225,85 +263,186 @@ def tile_groupqueryattention_pa_kernel(
         def out_view(out, h0):
             return out[0, h0 : h0 + 4, :, :].rearrange("h (p m) d -> p h m d", m=MT)
 
-        state = {"late": 0}
+        CHUNKS = ["q0", "q1", "q2", "q3", "k"]
+        N_BANKS = 8 * len(CHUNKS)
+        bank = {}
 
-        def normed_bank(m, key, tab, cps, c_sb, out, h0, group, offload):
-            acc = mx_bank(m, key)
-            prod = work.tile([P, 4, 4 * HALF], F32, tag="prod", bufs=6, name="prod")
+        plan_turn = {0: [("x3", 0, 0), ("x3", 0, 1)], 1: [("q1", 0, 0), ("q1", 0, 1)], 2: [("q1", 1, 0), ("q1", 1, 1)]}
+        plan_quant = {1: ["x2"], 3: ["x3"], 5: ["q1"]}
+        for start, name in ((6, "q2"), (10, "v"), (14, "q3"), (18, "k")):
+            for j in range(4):
+                plan_turn[start + j] = [(name, j // 2, j % 2)]
+            plan_quant[start + QLAG] = [name]
+        v_steps = {V0 + VSTEP * j: j for j in range(8)}
+        k_table_steps = {22: 0, 23: 2, 24: 4, 25: 6}
+        c_copy_steps = {3: 0, 4: 1}
+
+        def kind(i):
+            if i in P_SET:
+                return "P"
+            if i in O_SET:
+                return "O"
+            return "V"
+
+        def multiply(i):
+            bank[i] = {"acc": mx_bank(i % 8, CHUNKS[i // 8])}
+
+        def products(i):
+            b = bank[i]
+            tab = tab_k if i >= 32 else tab_q
+            b["prod"] = work.tile([P, 4, 4 * HALF], F32, tag="prod", bufs=6, name="prod")
             nc.vector.tensor_tensor(
-                out=prod[:].rearrange("p h (k d) -> p h k d", k=2),
-                in0=tab[:, m, :].rearrange("p (k d) -> p k d", k=2).unsqueeze(1).to_broadcast([P, 4, 2, DH]),
-                in1=acc[:].rearrange("p (h d) -> p h d", h=4).unsqueeze(2).to_broadcast([P, 4, 2, DH]),
+                out=b["prod"][:].rearrange("p h (k d) -> p h k d", k=2),
+                in0=tab[:, i % 8, :].rearrange("p (k d) -> p k d", k=2).unsqueeze(1).to_broadcast([P, 4, 2, DH]),
+                in1=b["acc"][:].rearrange("p (h d) -> p h d", h=4).unsqueeze(2).to_broadcast([P, 4, 2, DH]),
                 op=ALU.mult,
             )
+
+        def squares(i):
+            b = bank[i]
             ss = work.tile([P, 4], F32, tag="ss", bufs=6, name="ss")
-            junk = work.tile([P, DH], F32, tag="junk", bufs=2, name="junk")
+            junk = work.tile([P, 4, DH], F32, tag="junk", bufs=1, name="junk")
             for h in range(4):
-                nc.scalar.activation(out=junk[:], in_=acc[:, h * DH : (h + 1) * DH], func=ACT.Square,
+                nc.scalar.activation(out=junk[:, h, :], in_=b["acc"][:, h * DH : (h + 1) * DH], func=ACT.Square,
                                      accum_out=ss[:, h : h + 1])
-            rinv = work.tile([P, 4], F32, tag="rinv", bufs=6, name="rinv")
-            nc.scalar.activation(out=rinv[:], in_=ss[:], func=ACT.Abs_reciprocal_sqrt, bias=EPS, scale=1.0 / DH)
-            prod4 = prod[:].rearrange("p h (k e) -> p h k e", k=4)
-            rot = work.tile([P, 4, DH], F32, tag="rot", bufs=6, name="rot")
-            nc.gpsimd.tensor_tensor(
-                out=rot[:].rearrange("p h (t e) -> p h t e", t=2),
-                in0=prod4[:, :, 0:4:3, :], in1=prod4[:, :, 1:3, :], op=ALU.add,
-            )
-            mm = m % group
-            if mm == 0:
-                state["o"] = work.tile([P, 4, group, DH], F32, tag="o", bufs=4, name="o")
-            o = state["o"]
-            if offload:
-                scaled = work.tile([P, 4, DH], F32, tag="scaled", bufs=3, name="scaled")
-                for h in range(4):
-                    nc.scalar.activation(out=scaled[:, h, :], in_=rot[:, h, :], func=ACT.Copy,
-                                         scale=rinv[:, h : h + 1])
-                nc.gpsimd.tensor_tensor(out=o[:, :, mm, :], in0=scaled[:],
-                                        in1=c_sb[:, m, :].unsqueeze(1).to_broadcast([P, 4, DH]), op=ALU.add)
-            else:
-                for h in range(4):
-                    nc.vector.scalar_tensor_tensor(
-                        out=o[:, h, mm, :], in0=rot[:, h, :], scalar=rinv[:, h : h + 1],
-                        in1=cps[m // 4][:, m % 4, :], op0=ALU.mult, op1=ALU.add,
-                    )
-            if mm == group - 1:
-                nc.sync.dma_start(out=out_view(out, h0)[:, :, m - mm : m + 1, :], in_=o[:])
+            b["rinv"] = work.tile([P, 4], F32, tag="rinv", bufs=6, name="rinv")
+            nc.scalar.activation(out=b["rinv"][:], in_=ss[:], func=ACT.Abs_reciprocal_sqrt, bias=EPS, scale=1.0 / DH)
 
-        def plain_bank(m):
-            acc = mx_bank(m, "v")
-            mm = m % 2
-            if mm == 0:
-                state["ov"] = work.tile([P, 4, 2, DH], F32, tag="ov", bufs=2, name="ov")
-            ov = state["ov"]
-            nc.scalar.copy(out=ov[:, :, mm, :], in_=acc[:].rearrange("p (h d) -> p h d", h=4))
-            if mm == 1:
-                nc.sync.dma_start(out=out_view(out_2, 0)[:, :, m - 1 : m + 1, :], in_=ov[:])
+        def add_terms(i):
+            b = bank[i]
+            prod4 = b["prod"][:].rearrange("p h (k e) -> p h k e", k=4)
+            b["rot"] = work.tile([P, 4, DH], F32, tag="rot", bufs=6, name="rot")
+            adder = nc.vector if i == N_BANKS - 1 else nc.gpsimd
+            adder.tensor_tensor(out=b["rot"][:].rearrange("p h (t e) -> p h t e", t=2),
+                                in0=prod4[:, :, 0:4:3, :], in1=prod4[:, :, 1:3, :], op=ALU.add)
 
-        prep_x(0, 256, True)
-        prep_w("q0", 256, True)
-        prep_x(1)
+        def add_terms_tensor(i):
+            b = bank[i]
+            prod4 = b["prod"][:].rearrange("p h (k e) -> p h k e", k=4)
+            b["rot"] = psum.tile([P, 4, DH], F32, tag="bank", bufs=6, name="rot_ps")
+            for j, ks in enumerate((slice(0, 4, 3), slice(1, 3))):
+                nc.tensor.matmul(out=b["rot"][:], lhsT=ident[:], rhs=prod4[:, :, ks, :], start=(j == 0), stop=(j == 1))
+
+        def group(i):
+            return 1 if i >= 38 else 2
+
+        pair_out = {}
+
+        def out_tile(i):
+            g = group(i)
+            if i // g * g not in pair_out:
+                pair_out[i // g * g] = [work.tile([P, 4, g, DH], F32, tag="o", bufs=4, name="o"), 0]
+            return pair_out[i // g * g][0]
+
+        def store(i):
+            g = group(i)
+            i0 = i // g * g
+            pair_out[i0][1] = pair_out[i0][1] + 1
+            if pair_out[i0][1] == g:
+                out, h0, m = (out_1, 0, i0 % 8) if i0 >= 32 else (out_0, 4 * (i0 // 8), i0 % 8)
+                nc.sync.dma_start(out=out_view(out, h0)[:, :, m : m + g, :], in_=pair_out[i0][0][:])
+
+        def last_vector(i):
+            b, o = bank[i], out_tile(i)
+            cps = c_banks["k" if i >= 32 else "q"][(i % 8) // 4]
+            for h in range(4):
+                nc.vector.scalar_tensor_tensor(out=o[:, h, i % group(i), :], in0=b["rot"][:, h, :], scalar=b["rinv"][:, h : h + 1],
+                                               in1=cps[:, i % 4, :], op0=ALU.mult, op1=ALU.add)
+            store(i)
+
+        def scale_scalar(i):
+            b = bank[i]
+            b["scaled"] = work.tile([P, 4, DH], F32, tag="scaled", bufs=3, name="scaled")
+            for h in range(4):
+                nc.scalar.activation(out=b["scaled"][:, h, :], in_=b["rot"][:, h, :], func=ACT.Copy, scale=b["rinv"][:, h : h + 1])
+
+        def shift_gpsimd(i):
+            o = out_tile(i)
+            c_sb = c_k if i >= 32 else c_q
+            nc.gpsimd.tensor_tensor(out=o[:, :, i % group(i), :], in0=bank[i]["scaled"][:],
+                                    in1=c_sb[:, i % 8, :].unsqueeze(1).to_broadcast([P, 4, DH]), op=ALU.add)
+            store(i)
+
+        v_tiles = {}
+
+        def copy_v(m, acc):
+            if m % 2 == 0:
+                v_tiles["o"] = work.tile([P, 4, 2, DH], F32, tag="ov", bufs=2, name="ov")
+            nc.scalar.copy(out=v_tiles["o"][:, :, m % 2, :], in_=acc[:].rearrange("p (h d) -> p h d", h=4))
+            if m % 2 == 1:
+                nc.sync.dma_start(out=out_view(out_2, 0)[:, :, m - 1 : m + 1, :], in_=v_tiles["o"][:])
+
+        operand("x0", [None])
+        operand("q0", [None, None])
+        tp0 = turn_x_tile(0)
+        finish_x_tile(0, tp0)
+        bc4 = spread_vectors()
+        gains(bc4)
+        for g in range(2):
+            turn("q0", 0, g)
+            turn("q0", 1, g)
+            copy_out("q0")
+            copy_out("q0", True)
+            quantise("q0", 512 * g, 512 * (g + 1))
+        for lo, hi in ((0, 1), (1, 3), (3, MT)):
+            for step in tab_steps(nc.gpsimd, tab_q, 0, lo, hi):
+                step()
+        multiply(0)
+        tp1 = turn_x_tile(1)
+        finish_x_tile(1, tp1)
+        multiply(1)
+        operand("x1", [x_sb[1]])
+        turn("x1", 0, 0)
+        copy_out("x1")
+        turn("x1", 0, 1)
+        copy_out("x1")
+        operand("x2", [x_sb[2]])
+        turn("x2", 0, 0)
+        turn("x2", 0, 1)
+        quantise("x1", 0, 512)
         trig_t = trig_transposed()
-        cps_q = c_tables(trig_t, 0, c_q)
-        main = ["q0", "q1", "q2", "q3", "k"]
-        extra = {(0, 1): lambda: prep_x(2), (0, 3): lambda: prep_x(3), (0, 4): lambda: prep_w("q1"),
-                 (0, 6): lambda: prep_w("v")}
-        cps_now = cps_q
-        for ci, key in enumerate(main):
-            if key == "k":
-                cps_now = c_tables(trig_t, 1, c_k)
-            for m in range(MT):
-                b = MT * ci + m
-                offload = b % OFFLOAD_EVERY == OFFLOAD_EVERY - 1 and b < 37
-                if key == "k":
-                    normed_bank(m, key, tab_k, cps_now, c_k, out_1, 0, 2 if m < 6 else 1, offload)
-                else:
-                    normed_bank(m, key, tab_q, cps_now, c_q, out_0, 4 * ci, 2, offload)
-                if (ci, m) in extra:
-                    extra[(ci, m)]()
-                if ci >= 1 and m == 2 and ci + 1 < len(main):
-                    prep_w(main[ci + 1])
-                if ci >= 1 and m in (1, 5):
-                    plain_bank(2 * (ci - 1) + (m - 1) // 4)
-                if ci in (1, 2) and m in (3, 7):
-                    tab_k_pair(trig_t, state["late"])
-                    state["late"] = state["late"] + 2
+        c_banks = {}
+        late_constants(bc4)
+        c_banks["q"] = c_tables(trig_t, 0)
+        pending_copy = ["x2", "x2"]
+        pending_v = []
+        for i in range(N_BANKS + 4):
+            while pending_copy:
+                copy_out(pending_copy.pop(0))
+            if i < N_BANKS:
+                products(i)
+                squares(i)
+                if kind(i) != "P":
+                    add_terms(i)
+            if pending_v:
+                copy_v(*pending_v.pop(0))
+            for j in range(N_BANKS):
+                if kind(j) == "V" and i == min(j + LAG_V, max(j, N_BANKS - 1)):
+                    last_vector(j)
+            for name in plan_quant.get(i, []):
+                quantise(name, 0, 512 if name[0] == "x" else 1024)
+            j = i - LAG_S
+            if 0 <= j < N_BANKS and kind(j) != "V":
+                scale_scalar(j)
+            j = i - LAG_G
+            if 0 <= j < N_BANKS and kind(j) != "V":
+                shift_gpsimd(j)
+            if i + AHEAD < N_BANKS:
+                multiply(i + AHEAD)
+            if i in v_steps:
+                pending_v.append((v_steps[i], mx_bank(v_steps[i], "v")))
+            if 0 <= i - 1 < N_BANKS and kind(i - 1) == "P":
+                add_terms_tensor(i - 1)
+            for name, s, g in plan_turn.get(i, []):
+                if name not in operands:
+                    operand(name, [x_sb[int(name[1])]] if name[0] == "x" else w_sb[name])
+                turn(name, s, g)
+                pending_copy.append(name)
+            if i in k_table_steps:
+                tab_k_pair(trig_t, k_table_steps[i])
+            if i == 31:
+                c_banks["k"] = c_tables(trig_t, 1)
+            if i in c_copy_steps:
+                c_copy(c_banks["q"], c_q, c_copy_steps[i])
+            if i in (32, 33):
+                c_copy(c_banks["k"], c_k, i - 32)

@@ -51,7 +51,7 @@ def tile_groupqueryattention_pa_kernel(
         w_sb = {}
 
         def load_x(pair):
-            t = const.tile([P, 2, KDIM], BF16, name="x_sb%d" % pair)
+            t = work.tile([P, 2, KDIM], BF16, tag="load", bufs=9, name="x_sb%d" % pair)
             nc.sync.dma_start(out=t[:], in_=x_view[:, 2 * pair : 2 * pair + 2, :])
             x_sb[pair] = t
 
@@ -70,7 +70,7 @@ def tile_groupqueryattention_pa_kernel(
         def load_w(key, w, row0):
             halves = []
             for hf in range(2):
-                t = const.tile([P, 2, KDIM], BF16, name="w_sb_%s_%d" % (key, hf))
+                t = work.tile([P, 2, KDIM], BF16, tag="load", bufs=9, name="w_sb_%s_%d" % (key, hf))
                 nc.sync.dma_start(
                     out=t[:],
                     in_=w[row0 + 256 * hf : row0 + 256 * (hf + 1), :].rearrange("(c p) k -> p c k", p=P),
@@ -95,8 +95,6 @@ def tile_groupqueryattention_pa_kernel(
             load_w("q1", wq, 512)
             load_w("v", wv, 0)
             load_w("q2", wq, 1024)
-            load_w("q3", wq, 1536)
-            load_w("k", wk, 0)
 
         ident = const.tile([P, P], F32, name="ident")
         make_identity(nc, ident[:])
@@ -199,7 +197,7 @@ def tile_groupqueryattention_pa_kernel(
             rows = 256 * len(srcs)
             operands[name] = {
                 "srcs": srcs,
-                "grouped": work.tile([P, 8 * rows], BF16, tag="grouped", bufs=3, name="grouped", align_bytes=64),
+                "grouped": work.tile([P, 8 * rows], BF16, tag="grouped", bufs=2, name="grouped", align_bytes=64),
                 "codes": const.tile([P, 2 * rows], U32, name="codes_" + name, align_bytes=64),
                 "scales": const.tile([P, 2 * rows], U8, name="scales_" + name, align_bytes=64),
                 "banks": [],
@@ -290,7 +288,7 @@ def tile_groupqueryattention_pa_kernel(
         def products(i):
             b = bank[i]
             tab = tab_k if i >= 32 else tab_q
-            b["prod"] = work.tile([P, 4, 4 * HALF], F32, tag="prod", bufs=6, name="prod")
+            b["prod"] = work.tile([P, 4, 4 * HALF], F32, tag="prod", bufs=5, name="prod")
             nc.vector.tensor_tensor(
                 out=b["prod"][:].rearrange("p h (k d) -> p h k d", k=2),
                 in0=tab[:, i % 8, :].rearrange("p (k d) -> p k d", k=2).unsqueeze(1).to_broadcast([P, 4, 2, DH]),
@@ -324,14 +322,14 @@ def tile_groupqueryattention_pa_kernel(
                 nc.tensor.matmul(out=b["rot"][:], lhsT=ident[:], rhs=prod4[:, :, ks, :], start=(j == 0), stop=(j == 1))
 
         def group(i):
-            return 1 if i >= 38 else 2
+            return 4 if i < 36 else 2 if i < 38 else 1
 
         pair_out = {}
 
         def out_tile(i):
             g = group(i)
             if i // g * g not in pair_out:
-                pair_out[i // g * g] = [work.tile([P, 4, g, DH], F32, tag="o", bufs=4, name="o"), 0]
+                pair_out[i // g * g] = [work.tile([P, 4, g, DH], F32, tag="o4" if g == 4 else "o", bufs=4 if g == 4 else 3, name="o"), 0]
             return pair_out[i // g * g][0]
 
         def store(i):
@@ -438,6 +436,10 @@ def tile_groupqueryattention_pa_kernel(
                     operand(name, [x_sb[int(name[1])]] if name[0] == "x" else w_sb[name])
                 turn(name, s, g)
                 pending_copy.append(name)
+            if i == 3:
+                load_w("q3", wq, 1536)
+            if i == 4:
+                load_w("k", wk, 0)
             if i in k_table_steps:
                 tab_k_pair(trig_t, k_table_steps[i])
             if i == 31:

@@ -28,6 +28,7 @@ O_SET = range(1, 37, 4)
 V0 = 17
 VSTEP = 2
 QLAG = 6
+Q_TABLE_PARTS = ((0, 1), (1, 3), (3, 8))
 
 
 def tile_groupqueryattention_pa_kernel(
@@ -39,8 +40,10 @@ def tile_groupqueryattention_pa_kernel(
         work = ctx.enter_context(tc.tile_pool(name="work", bufs=1))
         psum = ctx.enter_context(tc.psum_pool(name="psum", bufs=1))
 
-        vec_rows = const.tile([P, 4 * DH], BF16, name="vec_rows")
-        nc.vector.memset(vec_rows[:], 0.0)
+        rows = const.tile([P, 4, 2 * DH], BF16, name="rows")
+        nc.vector.memset(rows[:], 0.0)
+        nc.vector.memset(rows[32:33, 0, :], 1.0)
+        nc.vector.memset(rows[32:33, 0, HALF:DH], -1.0)
         cos_sb = const.tile([P, MT, DH], BF16, name="cos_sb")
         sin_sb = const.tile([P, MT, DH], BF16, name="sin_sb")
 
@@ -81,10 +84,9 @@ def tile_groupqueryattention_pa_kernel(
         with tc.manual_schedule(engines={mybir.EngineType.SP}):
             load_x_tile(0)
             load_w_by_k("q0", wq, 0, 0)
-            for j, vec in enumerate((q_scale, q_shift, k_scale, k_shift)):
-                nc.sync.dma_start(
-                    out=vec_rows[0:1, j * DH : (j + 1) * DH], in_=vec.rearrange("(o d) -> o d", o=1)
-                )
+            nc.sync.dma_start(out=rows[0:1, 0, DH:], in_=q_scale.rearrange("(o d) -> o d", o=1))
+            for j, vec in enumerate((k_scale, q_shift, k_shift)):
+                nc.sync.dma_start(out=rows[0:1, 1 + j, 0:DH], in_=vec.rearrange("(o d) -> o d", o=1))
             load_w_by_k("q0", wq, 0, 1)
             nc.sync.dma_start(out=cos_sb[:], in_=cos_thetas.rearrange("(p m) d -> p m d", m=MT))
             nc.sync.dma_start(out=sin_sb[:], in_=sin_thetas.rearrange("(p m) d -> p m d", m=MT))
@@ -106,32 +108,27 @@ def tile_groupqueryattention_pa_kernel(
         nc.vector.memset(warm[:], 1.0)
         nc.scalar.activation(out=warm[:], in_=warm[:], func=ACT.Abs_reciprocal_sqrt)
 
-        gain4 = const.tile([P, 2, 4 * HALF], F32, name="gain4")
-        vec2 = const.tile([P, 2, 2, 4 * HALF], F32, name="vec2")
-        dmat = const.tile([P, 8, DH], BF16, name="dmat")
+        dmat = const.tile([P, 6, DH], BF16, name="dmat")
         unit2 = const.tile([P, 2, DH], BF16, name="unit2")
 
         def spread_vectors():
-            bc_ps = psum.tile([P, 512], F32, tag="bank", bufs=6, name="bc_ps")
-            nc.tensor.matmul(out=bc_ps[:], lhsT=ones[:], rhs=vec_rows[:], start=True, stop=True)
-            return bc_ps[:].rearrange("p (t s d) -> p t s d", t=2, s=2)
+            nc.vector.tensor_copy(out=rows[0:1, 0, 0:HALF], in_=rows[0:1, 0, DH : DH + HALF])
+            nc.vector.tensor_scalar_mul(out=rows[0:1, 0, HALF:DH], in0=rows[0:1, 0, DH + HALF :], scalar1=-1.0)
+            nc.vector.tensor_scalar_mul(out=rows[0:1, 1:4, DH : DH + HALF], in0=rows[0:1, 1:4, HALF:DH], scalar1=-1.0)
+            nc.vector.tensor_copy(out=rows[0:1, 1:4, DH + HALF :], in_=rows[0:1, 1:4, 0:HALF])
+            banks = []
+            for j in range(2):
+                spread = psum.tile([P, 2, 2 * DH], F32, tag="cps", bufs=2, name="spread")
+                nc.tensor.matmul(out=spread[:], lhsT=ones[:], rhs=rows[:, 2 * j : 2 * j + 2, :], start=True, stop=True)
+                banks.append(spread)
+            return banks
 
-        def gains(bc4):
-            nc.vector.tensor_scalar_add(out=gain4[:, :, 0:64], in0=bc4[:, :, 0, 0:64], scalar1=1.0)
-            nc.vector.tensor_scalar(
-                out=gain4[:, :, 64:128], in0=bc4[:, :, 0, 64:128], scalar1=-1.0, scalar2=-1.0,
-                op0=ALU.mult, op1=ALU.add,
-            )
-            nc.vector.tensor_scalar_add(out=gain4[:, :, 128:256], in0=bc4[:, :, 0, :], scalar1=1.0)
-
-        def late_constants(bc4):
-            nc.vector.tensor_copy(out=vec2[:, :, :, 0:128], in_=bc4[:, :, :, :])
-            nc.vector.tensor_scalar_mul(out=vec2[:, :, :, 128:192], in0=bc4[:, :, :, 64:128], scalar1=-1.0)
-            nc.vector.tensor_copy(out=vec2[:, :, :, 192:256], in_=bc4[:, :, :, 0:64])
-            nc.vector.tensor_tensor(
-                out=dmat[:], in0=ident[:].unsqueeze(1).to_broadcast([P, 8, DH]),
-                in1=vec2[:].rearrange("p t s (j d) -> p (t s j) d", j=2), op=ALU.mult,
-            )
+        def late_constants(banks):
+            for j0, n, src in ((0, 2, banks[0][:, 1, :]), (2, 4, banks[1][:].rearrange("p a d -> p (a d)"))):
+                nc.vector.tensor_tensor(
+                    out=dmat[:, j0 : j0 + n, :], in0=ident_bf[:].unsqueeze(1).to_broadcast([P, n, DH]),
+                    in1=src.rearrange("p (n d) -> p n d", n=n), op=ALU.mult,
+                )
             nc.vector.tensor_copy(out=unit2[:, 0, :], in_=ident_bf[:])
             nc.vector.tensor_scalar_mul(out=unit2[:, 1, 0:64], in0=ident_bf[:, 0:64], scalar1=-1.0)
             nc.vector.tensor_copy(out=unit2[:, 1, 64:128], in_=ident_bf[:, 64:128])
@@ -139,16 +136,11 @@ def tile_groupqueryattention_pa_kernel(
         def over_m(ap, n_m):
             return ap.unsqueeze(1).to_broadcast([P, n_m, ap.shape[1]])
 
-        def tab_steps(eng, tab, t, m0, m1):
+        def q_table(gain, m0, m1):
             ms = slice(m0, m1)
-            return [
-                lambda: eng.tensor_tensor(out=tab[:, ms, 0:64], in0=cos_sb[:, ms, 0:64],
-                                          in1=over_m(gain4[:, t, 0:64], m1 - m0), op=ALU.mult),
-                lambda: eng.tensor_tensor(out=tab[:, ms, 64:192], in0=sin_sb[:, ms, :],
-                                          in1=over_m(gain4[:, t, 64:192], m1 - m0), op=ALU.mult),
-                lambda: eng.tensor_tensor(out=tab[:, ms, 192:256], in0=cos_sb[:, ms, 64:128],
-                                          in1=over_m(gain4[:, t, 192:256], m1 - m0), op=ALU.mult),
-            ]
+            for src, cols in ((cos_sb[:, ms, 0:64], slice(0, 64)), (sin_sb[:, ms, :], slice(64, 192)),
+                              (cos_sb[:, ms, 64:128], slice(192, 256))):
+                nc.gpsimd.tensor_tensor(out=tab_q[:, ms, cols], in0=src, in1=over_m(gain[:, cols], m1 - m0), op=ALU.mult)
 
         def trig_transposed():
             trig_t = const.tile([P, 2, MT, P], BF16, name="trig_t")
@@ -164,9 +156,9 @@ def tile_groupqueryattention_pa_kernel(
             for j in range(2):
                 cps = psum.tile([P, 4, DH], F32, tag="cps", bufs=2, name="cps")
                 for i in range(4):
-                    nc.tensor.matmul(out=cps[:, i, :], lhsT=trig_t[:, 0, 4 * j + i, :], rhs=dmat[:, 4 * t + 2, :],
+                    nc.tensor.matmul(out=cps[:, i, :], lhsT=trig_t[:, 0, 4 * j + i, :], rhs=dmat[:, 2 + 2 * t, :],
                                      start=True, stop=False)
-                    nc.tensor.matmul(out=cps[:, i, :], lhsT=trig_t[:, 1, 4 * j + i, :], rhs=dmat[:, 4 * t + 3, :],
+                    nc.tensor.matmul(out=cps[:, i, :], lhsT=trig_t[:, 1, 4 * j + i, :], rhs=dmat[:, 3 + 2 * t, :],
                                      start=False, stop=True)
                 banks.append(cps)
             return banks
@@ -182,7 +174,7 @@ def tile_groupqueryattention_pa_kernel(
                     nc.tensor.matmul(out=out_j, lhsT=trig_t[:, j, m0 + i, :],
                                      rhs=unit2[:, j, :].rearrange("p (k e) -> p k e", k=2), start=True, stop=False)
                     nc.tensor.matmul(out=out_j, lhsT=trig_t[:, j, m0 + i, :],
-                                     rhs=dmat[:, 4 + j, :].rearrange("p (k e) -> p k e", k=2), start=False, stop=True)
+                                     rhs=dmat[:, j, :].rearrange("p (k e) -> p k e", k=2), start=False, stop=True)
             nc.scalar.copy(out=tab_k[:, m0 : m0 + 2, :], in_=tps[:])
 
         tab_q = const.tile([P, MT, 4 * HALF], F32, name="tab_q")
@@ -374,17 +366,17 @@ def tile_groupqueryattention_pa_kernel(
         operand("q0", [None, None])
         tp0 = turn_x_tile(0)
         finish_x_tile(0, tp0)
-        bc4 = spread_vectors()
-        gains(bc4)
+        spread = spread_vectors()
+        gain = const.tile([P, 2 * DH], F32, name="gain")
+        nc.vector.tensor_copy(out=gain[:], in_=spread[0][:, 0, :])
         for g in range(2):
             turn("q0", 0, g)
             turn("q0", 1, g)
             copy_out("q0")
             copy_out("q0", True)
             quantise("q0", 512 * g, 512 * (g + 1))
-        for lo, hi in ((0, 1), (1, 3), (3, MT)):
-            for step in tab_steps(nc.gpsimd, tab_q, 0, lo, hi):
-                step()
+        for lo, hi in Q_TABLE_PARTS:
+            q_table(gain[:], lo, hi)
         multiply(0)
         tp1 = turn_x_tile(1)
         finish_x_tile(1, tp1)
@@ -393,14 +385,14 @@ def tile_groupqueryattention_pa_kernel(
         turn("x1", 0, 0)
         copy_out("x1")
         turn("x1", 0, 1)
-        copy_out("x1")
+        copy_out("x1", True)
         operand("x2", [x_sb[2]])
         turn("x2", 0, 0)
         turn("x2", 0, 1)
         quantise("x1", 0, 512)
         trig_t = trig_transposed()
         c_banks = {}
-        late_constants(bc4)
+        late_constants(spread)
         c_banks["q"] = c_tables(trig_t, 0)
         pending_copy = ["x2", "x2"]
         pending_v = []

@@ -23,7 +23,6 @@ AHEAD = 2
 LAG_V = 2
 LAG_S = 2
 LAG_G = 3
-P_SET = range(0, 0, 3)
 O_SET = range(1, 37, 4)
 V0 = 17
 VSTEP = 2
@@ -129,9 +128,9 @@ def tile_groupqueryattention_pa_kernel(
                     out=dmat[:, j0 : j0 + n, :], in0=ident_bf[:].unsqueeze(1).to_broadcast([P, n, DH]),
                     in1=src.rearrange("p (n d) -> p n d", n=n), op=ALU.mult,
                 )
-            nc.vector.tensor_copy(out=unit2[:, 0, :], in_=ident_bf[:])
-            nc.vector.tensor_scalar_mul(out=unit2[:, 1, 0:64], in0=ident_bf[:, 0:64], scalar1=-1.0)
-            nc.vector.tensor_copy(out=unit2[:, 1, 64:128], in_=ident_bf[:, 64:128])
+            nc.gpsimd.tensor_copy(out=unit2[:, 0, :], in_=ident_bf[:])
+            nc.gpsimd.tensor_scalar_mul(out=unit2[:, 1, 0:64], in0=ident_bf[:, 0:64], scalar1=-1.0)
+            nc.gpsimd.tensor_copy(out=unit2[:, 1, 64:128], in_=ident_bf[:, 64:128])
 
         def over_m(ap, n_m):
             return ap.unsqueeze(1).to_broadcast([P, n_m, ap.shape[1]])
@@ -268,8 +267,6 @@ def tile_groupqueryattention_pa_kernel(
         c_copy_steps = {3: 0, 4: 1}
 
         def kind(i):
-            if i in P_SET:
-                return "P"
             if i in O_SET:
                 return "O"
             return "V"
@@ -306,13 +303,6 @@ def tile_groupqueryattention_pa_kernel(
             adder.tensor_tensor(out=b["rot"][:].rearrange("p h (t e) -> p h t e", t=2),
                                 in0=prod4[:, :, 0:4:3, :], in1=prod4[:, :, 1:3, :], op=ALU.add)
 
-        def add_terms_tensor(i):
-            b = bank[i]
-            prod4 = b["prod"][:].rearrange("p h (k e) -> p h k e", k=4)
-            b["rot"] = psum.tile([P, 4, DH], F32, tag="bank", bufs=6, name="rot_ps")
-            for j, ks in enumerate((slice(0, 4, 3), slice(1, 3))):
-                nc.tensor.matmul(out=b["rot"][:], lhsT=ident[:], rhs=prod4[:, :, ks, :], start=(j == 0), stop=(j == 1))
-
         def group(i):
             return 4 if i < 36 else 2 if i < 38 else 1
 
@@ -321,7 +311,7 @@ def tile_groupqueryattention_pa_kernel(
         def out_tile(i):
             g = group(i)
             if i // g * g not in pair_out:
-                pair_out[i // g * g] = [work.tile([P, 4, g, DH], F32, tag="o4" if g == 4 else "o", bufs=4 if g == 4 else 3, name="o"), 0]
+                pair_out[i // g * g] = [work.tile([P, 4, g, DH], F32, tag="o4" if g == 4 else "o", bufs=5 if g == 4 else 3, name="o"), 0]
             return pair_out[i // g * g][0]
 
         def store(i):
@@ -330,7 +320,9 @@ def tile_groupqueryattention_pa_kernel(
             pair_out[i0][1] = pair_out[i0][1] + 1
             if pair_out[i0][1] == g:
                 out, h0, m = (out_1, 0, i0 % 8) if i0 >= 32 else (out_0, 4 * (i0 // 8), i0 % 8)
-                nc.sync.dma_start(out=out_view(out, h0)[:, :, m : m + g, :], in_=pair_out[i0][0][:])
+                step = 2 if i == N_BANKS - 1 else 4
+                for h in range(0, 4, step):
+                    nc.sync.dma_start(out=out_view(out, h0)[:, h : h + step, m : m + g, :], in_=pair_out[i0][0][:, h : h + step, :, :])
 
         def last_vector(i):
             b, o = bank[i], out_tile(i)
@@ -356,22 +348,23 @@ def tile_groupqueryattention_pa_kernel(
         v_tiles = {}
 
         def copy_v(m, acc):
-            if m % 2 == 0:
-                v_tiles["o"] = work.tile([P, 4, 2, DH], F32, tag="ov", bufs=2, name="ov")
-            nc.scalar.copy(out=v_tiles["o"][:, :, m % 2, :], in_=acc[:].rearrange("p (h d) -> p h d", h=4))
-            if m % 2 == 1:
-                nc.sync.dma_start(out=out_view(out_2, 0)[:, :, m - 1 : m + 1, :], in_=v_tiles["o"][:])
+            if m % 4 == 0:
+                v_tiles["o"] = work.tile([P, 4, 4, DH], F32, tag="o4", bufs=5, name="ov")
+            nc.scalar.copy(out=v_tiles["o"][:, :, m % 4, :], in_=acc[:].rearrange("p (h d) -> p h d", h=4))
+            if m % 4 == 3:
+                nc.sync.dma_start(out=out_view(out_2, 0)[:, :, m - 3 : m + 1, :], in_=v_tiles["o"][:])
 
         operand("x0", [None])
         operand("q0", [None, None])
         tp0 = turn_x_tile(0)
         finish_x_tile(0, tp0)
-        spread = spread_vectors()
         gain = const.tile([P, 2 * DH], F32, name="gain")
-        nc.vector.tensor_copy(out=gain[:], in_=spread[0][:, 0, :])
         for g in range(2):
             turn("q0", 0, g)
             turn("q0", 1, g)
+            if g == 0:
+                spread = spread_vectors()
+                nc.vector.tensor_copy(out=gain[:], in_=spread[0][:, 0, :])
             copy_out("q0")
             copy_out("q0", True)
             quantise("q0", 512 * g, 512 * (g + 1))
@@ -381,6 +374,7 @@ def tile_groupqueryattention_pa_kernel(
         tp1 = turn_x_tile(1)
         finish_x_tile(1, tp1)
         multiply(1)
+        trig_t = trig_transposed()
         operand("x1", [x_sb[1]])
         turn("x1", 0, 0)
         copy_out("x1")
@@ -390,7 +384,6 @@ def tile_groupqueryattention_pa_kernel(
         turn("x2", 0, 0)
         turn("x2", 0, 1)
         quantise("x1", 0, 512)
-        trig_t = trig_transposed()
         c_banks = {}
         late_constants(spread)
         c_banks["q"] = c_tables(trig_t, 0)
@@ -402,8 +395,7 @@ def tile_groupqueryattention_pa_kernel(
             if i < N_BANKS:
                 products(i)
                 squares(i)
-                if kind(i) != "P":
-                    add_terms(i)
+                add_terms(i)
             if pending_v:
                 copy_v(*pending_v.pop(0))
             for j in range(N_BANKS):
@@ -421,8 +413,6 @@ def tile_groupqueryattention_pa_kernel(
                 multiply(i + AHEAD)
             if i in v_steps:
                 pending_v.append((v_steps[i], mx_bank(v_steps[i], "v")))
-            if 0 <= i - 1 < N_BANKS and kind(i - 1) == "P":
-                add_terms_tensor(i - 1)
             for name, s, g in plan_turn.get(i, []):
                 if name not in operands:
                     operand(name, [x_sb[int(name[1])]] if name[0] == "x" else w_sb[name])

@@ -20,8 +20,8 @@ MT = SEQ // P
 EPS = 1e-6
 FLOPS = 2 * SEQ * KDIM * 3072
 AHEAD = 2
-LAG_V = 2
-LAG_S = 2
+LAG_V = 3
+LAG_S = 1
 LAG_G = 3
 O_SET = range(1, 37, 4)
 V0 = 17
@@ -356,15 +356,17 @@ def tile_groupqueryattention_pa_kernel(
 
         operand("x0", [None])
         operand("q0", [None, None])
-        tp0 = turn_x_tile(0)
-        finish_x_tile(0, tp0)
         gain = const.tile([P, 2 * DH], F32, name="gain")
+        with tc.manual_schedule(engines={mybir.EngineType.PE}):
+            tp0 = turn_x_tile(0)
+            finish_x_tile(0, tp0)
+            turn("q0", 0, 0)
+            turn("q0", 1, 0)
+            spread = spread_vectors()
+            turn("q0", 0, 1)
+            turn("q0", 1, 1)
+        nc.vector.tensor_copy(out=gain[:], in_=spread[0][:, 0, :])
         for g in range(2):
-            turn("q0", 0, g)
-            turn("q0", 1, g)
-            if g == 0:
-                spread = spread_vectors()
-                nc.vector.tensor_copy(out=gain[:], in_=spread[0][:, 0, :])
             copy_out("q0")
             copy_out("q0", True)
             quantise("q0", 512 * g, 512 * (g + 1))
@@ -374,7 +376,6 @@ def tile_groupqueryattention_pa_kernel(
         tp1 = turn_x_tile(1)
         finish_x_tile(1, tp1)
         multiply(1)
-        trig_t = trig_transposed()
         operand("x1", [x_sb[1]])
         turn("x1", 0, 0)
         copy_out("x1")
@@ -384,6 +385,7 @@ def tile_groupqueryattention_pa_kernel(
         turn("x2", 0, 0)
         turn("x2", 0, 1)
         quantise("x1", 0, 512)
+        trig_t = trig_transposed()
         c_banks = {}
         late_constants(spread)
         c_banks["q"] = c_tables(trig_t, 0)

@@ -23,10 +23,13 @@ AHEAD = 2
 LAG_V = 3
 LAG_S = 1
 LAG_G = 3
-O_SET = range(1, 37, 4)
+O_SET = range(5, 37, 4)
 V0 = 17
 VSTEP = 2
 QLAG = 6
+FIRST_CLOCK = 3
+SECOND_CLOCK = 0
+CLOCKED = ()
 Q_TABLE_PARTS = ((0, 1), (1, 3), (3, 8))
 
 
@@ -39,6 +42,8 @@ def tile_groupqueryattention_pa_kernel(
         work = ctx.enter_context(tc.tile_pool(name="work", bufs=1))
         psum = ctx.enter_context(tc.psum_pool(name="psum", bufs=1))
 
+        zeros = const.tile([P, P], F32, name="zeros")
+        nc.vector.memset(zeros[:], 0.0)
         rows = const.tile([P, 4, 2 * DH], BF16, name="rows")
         nc.vector.memset(rows[:], 0.0)
         nc.vector.memset(rows[32:33, 0, :], 1.0)
@@ -163,7 +168,7 @@ def tile_groupqueryattention_pa_kernel(
             return banks
 
         def c_copy(banks, c_sb, j):
-            nc.scalar.copy(out=c_sb[:, 4 * j : 4 * j + 4, :], in_=banks[j][:])
+            nc.scalar.copy(out=c_sb[:, j, :], in_=banks[j][:, 1, :])
 
         def tab_k_pair(trig_t, m0):
             tps = psum.tile([P, 2, 4 * HALF], F32, tag="bank", bufs=6, name="tabps")
@@ -178,8 +183,8 @@ def tile_groupqueryattention_pa_kernel(
 
         tab_q = const.tile([P, MT, 4 * HALF], F32, name="tab_q")
         tab_k = const.tile([P, MT, 4 * HALF], F32, name="tab_k")
-        c_q = const.tile([P, MT, DH], F32, name="c_q")
-        c_k = const.tile([P, MT, DH], F32, name="c_k")
+        c_q = const.tile([P, 2, DH], F32, name="c_q")
+        c_k = const.tile([P, 2, DH], F32, name="c_k")
 
 
         operands = {}
@@ -194,8 +199,13 @@ def tile_groupqueryattention_pa_kernel(
                 "banks": [],
             }
 
-        def turn(name, s, g, tag="tp"):
+        def keep_clock(out):
+            nc.tensor.matmul(out=out, lhsT=zeros[:], rhs=zeros[:], start=True, stop=True)
+
+        def turn(name, s, g):
             tp = psum.tile([P, 2, 256], F32, tag="bank", bufs=6, name="tp")
+            if name in CLOCKED:
+                keep_clock(tp[:, 0, 0:P])
             for c in range(2):
                 if name == "q0":
                     words = w_first[g][:, 2 * s + c, :].bitcast(F32)
@@ -207,6 +217,8 @@ def tile_groupqueryattention_pa_kernel(
 
         def turn_x_tile(m):
             tp = psum.tile([P, 2, 2, P], F32, tag="bank", bufs=6, name="tp")
+            for n in range(FIRST_CLOCK if m == 0 else SECOND_CLOCK):
+                keep_clock(tp[:, 0, 0, :])
             words = x_first[m][:].bitcast(F32)
             for g in range(2):
                 for u in range(2):
@@ -264,7 +276,7 @@ def tile_groupqueryattention_pa_kernel(
             plan_quant[start + QLAG] = [name]
         v_steps = {V0 + VSTEP * j: j for j in range(8)}
         k_table_steps = {22: 0, 23: 2, 24: 4, 25: 6}
-        c_copy_steps = {3: 0, 4: 1}
+        c_copy_steps = {6: 0, 7: 1}
 
         def kind(i):
             if i in O_SET:
@@ -342,7 +354,7 @@ def tile_groupqueryattention_pa_kernel(
             o = out_tile(i)
             c_sb = c_k if i >= 32 else c_q
             nc.gpsimd.tensor_tensor(out=o[:, :, i % group(i), :], in0=bank[i]["scaled"][:],
-                                    in1=c_sb[:, i % 8, :].unsqueeze(1).to_broadcast([P, 4, DH]), op=ALU.add)
+                                    in1=c_sb[:, i % 8 // 4, :].unsqueeze(1).to_broadcast([P, 4, DH]), op=ALU.add)
             store(i)
 
         v_tiles = {}
@@ -365,7 +377,7 @@ def tile_groupqueryattention_pa_kernel(
             spread = spread_vectors()
             turn("q0", 0, 1)
             turn("q0", 1, 1)
-        nc.vector.tensor_copy(out=gain[:], in_=spread[0][:, 0, :])
+        nc.scalar.copy(out=gain[:], in_=spread[0][:, 0, :])
         for g in range(2):
             copy_out("q0")
             copy_out("q0", True)
@@ -380,7 +392,7 @@ def tile_groupqueryattention_pa_kernel(
         turn("x1", 0, 0)
         copy_out("x1")
         turn("x1", 0, 1)
-        copy_out("x1", True)
+        copy_out("x1")
         operand("x2", [x_sb[2]])
         turn("x2", 0, 0)
         turn("x2", 0, 1)
@@ -430,5 +442,5 @@ def tile_groupqueryattention_pa_kernel(
                 c_banks["k"] = c_tables(trig_t, 1)
             if i in c_copy_steps:
                 c_copy(c_banks["q"], c_q, c_copy_steps[i])
-            if i in (32, 33):
-                c_copy(c_banks["k"], c_k, i - 32)
+            if i == 32:
+                c_copy(c_banks["k"], c_k, 0)

@@ -289,7 +289,7 @@ def tile_groupqueryattention_pa_kernel(
         def products(i):
             b = bank[i]
             tab = tab_k if i >= 32 else tab_q
-            b["prod"] = work.tile([P, 4, 4 * HALF], F32, tag="prod", bufs=5, name="prod")
+            b["prod"] = work.tile([P, 4, 4 * HALF], F32, tag="prod", bufs=6, name="prod")
             nc.vector.tensor_tensor(
                 out=b["prod"][:].rearrange("p h (k d) -> p h k d", k=2),
                 in0=tab[:, i % 8, :].rearrange("p (k d) -> p k d", k=2).unsqueeze(1).to_broadcast([P, 4, 2, DH]),
@@ -299,12 +299,12 @@ def tile_groupqueryattention_pa_kernel(
 
         def squares(i):
             b = bank[i]
-            ss = work.tile([P, 4], F32, tag="ss", bufs=6, name="ss")
+            ss = work.tile([P, 4], F32, tag="ss", bufs=8, name="ss")
             junk = work.tile([P, 4, DH], F32, tag="junk", bufs=1, name="junk")
             for h in range(4):
                 nc.scalar.activation(out=junk[:, h, :], in_=b["acc"][:, h * DH : (h + 1) * DH], func=ACT.Square,
                                      accum_out=ss[:, h : h + 1])
-            b["rinv"] = work.tile([P, 4], F32, tag="rinv", bufs=6, name="rinv")
+            b["rinv"] = work.tile([P, 4], F32, tag="rinv", bufs=8, name="rinv")
             nc.scalar.activation(out=b["rinv"][:], in_=ss[:], func=ACT.Abs_reciprocal_sqrt, bias=EPS, scale=1.0 / DH)
 
         def add_terms(i):
@@ -346,7 +346,7 @@ def tile_groupqueryattention_pa_kernel(
 
         def scale_scalar(i):
             b = bank[i]
-            b["scaled"] = work.tile([P, 4, DH], F32, tag="scaled", bufs=3, name="scaled")
+            b["scaled"] = work.tile([P, 4, DH], F32, tag="scaled", bufs=4, name="scaled")
             for h in range(4):
                 nc.scalar.activation(out=b["scaled"][:, h, :], in_=b["rot"][:, h, :], func=ACT.Copy, scale=b["rinv"][:, h : h + 1])
 

from contextlib import ExitStack

import concourse.mybir as mybir
from concourse.masks import make_identity

F32 = mybir.dt.float32
BF16 = mybir.dt.bfloat16
U32 = mybir.dt.uint32
U8 = mybir.dt.uint8
E5X4 = mybir.dt.float8_e5m2_x4
ACT = mybir.ActivationFunctionType
ALU = mybir.AluOpType

P = 128
SEQ = 1024
KDIM = 1024
DH = 128
HALF = 64
MT = SEQ // P
EPS = 1e-6
FLOPS = 2 * SEQ * KDIM * 3072
AHEAD = 2
LAG_V = 3
LAG_S = 1
LAG_G = 3
O_SET = range(5, 37, 4)
V0 = 17
VSTEP = 2
QLAG = 6
FIRST_CLOCK = 3
SECOND_CLOCK = 0
CLOCKED = ()
Q_TABLE_PARTS = ((0, 1), (1, 3), (3, 8))


def tile_groupqueryattention_pa_kernel(
    tc, x, sin_thetas, cos_thetas, wq, wk, wv, q_scale, q_shift, k_scale, k_shift, out_0, out_1, out_2
):
    nc = tc.nc
    with ExitStack() as ctx:
        const = ctx.enter_context(tc.tile_pool(name="const", bufs=1))
        work = ctx.enter_context(tc.tile_pool(name="work", bufs=1))
        psum = ctx.enter_context(tc.psum_pool(name="psum", bufs=1))

        zeros = const.tile([P, P], F32, name="zeros")
        nc.vector.memset(zeros[:], 0.0)
        rows = const.tile([P, 4, 2 * DH], BF16, name="rows")
        nc.vector.memset(rows[:], 0.0)
        nc.vector.memset(rows[32:33, 0, :], 1.0)
        nc.vector.memset(rows[32:33, 0, HALF:DH], -1.0)
        cos_sb = const.tile([P, MT, DH], BF16, name="cos_sb")
        sin_sb = const.tile([P, MT, DH], BF16, name="sin_sb")

        x_view = x[0].rearrange("(p m) k -> p m k", m=MT)
        x_sb = {}
        x_first = []
        w_first = []
        w_sb = {}

        def load_x(pair):
            t = work.tile([P, 2, KDIM], BF16, tag="load", bufs=9, name="x_sb%d" % pair)
            nc.sync.dma_start(out=t[:], in_=x_view[:, 2 * pair : 2 * pair + 2, :])
            x_sb[pair] = t

        def load_x_tile(m):
            t = const.tile([P, KDIM], BF16, name="x_first%d" % m)
            nc.sync.dma_start(out=t[:], in_=x_view[:, m, :])
            x_first.append(t)

        def load_w_by_k(key, w, row0, g):
            t = const.tile([P, 4, 512], BF16, name="w_sb_%s_k%d" % (key, g))
            nc.sync.dma_start(
                out=t[:], in_=w[row0 : row0 + 512, 512 * g : 512 * (g + 1)].rearrange("(c p) k -> p c k", p=P)
            )
            w_first.append(t)

        def load_w(key, w, row0):
            halves = []
            for hf in range(2):
                t = work.tile([P, 2, KDIM], BF16, tag="load", bufs=9, name="w_sb_%s_%d" % (key, hf))
                nc.sync.dma_start(
                    out=t[:],
                    in_=w[row0 + 256 * hf : row0 + 256 * (hf + 1), :].rearrange("(c p) k -> p c k", p=P),
                )
                halves.append(t)
            w_sb[key] = halves

        with tc.manual_schedule(engines={mybir.EngineType.SP}):
            load_x_tile(0)
            load_w_by_k("q0", wq, 0, 0)
            nc.sync.dma_start(out=rows[0:1, 0, DH:], in_=q_scale.rearrange("(o d) -> o d", o=1))
            for j, vec in enumerate((k_scale, q_shift, k_shift)):
                nc.sync.dma_start(out=rows[0:1, 1 + j, 0:DH], in_=vec.rearrange("(o d) -> o d", o=1))
            load_w_by_k("q0", wq, 0, 1)
            nc.sync.dma_start(out=cos_sb[:], in_=cos_thetas.rearrange("(p m) d -> p m d", m=MT))
            nc.sync.dma_start(out=sin_sb[:], in_=sin_thetas.rearrange("(p m) d -> p m d", m=MT))
            load_x_tile(1)
            load_x(1)
            load_x(2)
            load_x(3)
            load_w("q1", wq, 512)
            load_w("v", wv, 0)
            load_w("q2", wq, 1024)

        ident = const.tile([P, P], F32, name="ident")
        make_identity(nc, ident[:])
        ident_bf = const.tile([P, P], BF16, name="ident_bf")
        make_identity(nc, ident_bf[:])
        ones = const.tile([P, P], BF16, name="ones")
        nc.vector.memset(ones[:], 1.0)
        warm = const.tile([P, 1], F32, name="warm")
        nc.vector.memset(warm[:], 1.0)
        nc.scalar.activation(out=warm[:], in_=warm[:], func=ACT.Abs_reciprocal_sqrt)

        dmat = const.tile([P, 6, DH], BF16, name="dmat")
        unit2 = const.tile([P, 2, DH], BF16, name="unit2")

        def spread_vectors():
            nc.vector.tensor_copy(out=rows[0:1, 0, 0:HALF], in_=rows[0:1, 0, DH : DH + HALF])
            nc.vector.tensor_scalar_mul(out=rows[0:1, 0, HALF:DH], in0=rows[0:1, 0, DH + HALF :], scalar1=-1.0)
            nc.vector.tensor_scalar_mul(out=rows[0:1, 1:4, DH : DH + HALF], in0=rows[0:1, 1:4, HALF:DH], scalar1=-1.0)
            nc.vector.tensor_copy(out=rows[0:1, 1:4, DH + HALF :], in_=rows[0:1, 1:4, 0:HALF])
            banks = []
            for j in range(2):
                spread = psum.tile([P, 2, 2 * DH], F32, tag="cps", bufs=2, name="spread")
                nc.tensor.matmul(out=spread[:], lhsT=ones[:], rhs=rows[:, 2 * j : 2 * j + 2, :], start=True, stop=True)
                banks.append(spread)
            return banks

        def late_constants(banks):
            for j0, n, src in ((0, 2, banks[0][:, 1, :]), (2, 4, banks[1][:].rearrange("p a d -> p (a d)"))):
                nc.vector.tensor_tensor(
                    out=dmat[:, j0 : j0 + n, :], in0=ident_bf[:].unsqueeze(1).to_broadcast([P, n, DH]),
                    in1=src.rearrange("p (n d) -> p n d", n=n), op=ALU.mult,
                )
            nc.gpsimd.tensor_copy(out=unit2[:, 0, :], in_=ident_bf[:])
            nc.gpsimd.tensor_scalar_mul(out=unit2[:, 1, 0:64], in0=ident_bf[:, 0:64], scalar1=-1.0)
            nc.gpsimd.tensor_copy(out=unit2[:, 1, 64:128], in_=ident_bf[:, 64:128])

        def over_m(ap, n_m):
            return ap.unsqueeze(1).to_broadcast([P, n_m, ap.shape[1]])

        def q_table(gain, m0, m1):
            ms = slice(m0, m1)
            for src, cols in ((cos_sb[:, ms, 0:64], slice(0, 64)), (sin_sb[:, ms, :], slice(64, 192)),
                              (cos_sb[:, ms, 64:128], slice(192, 256))):
                nc.gpsimd.tensor_tensor(out=tab_q[:, ms, cols], in0=src, in1=over_m(gain[:, cols], m1 - m0), op=ALU.mult)

        def trig_transposed():
            trig_t = const.tile([P, 2, MT, P], BF16, name="trig_t")
            for j, src in enumerate((cos_sb, sin_sb)):
                tps = psum.tile([P, MT, P], BF16, tag="bank", bufs=6, name="tps")
                for m in range(MT):
                    nc.tensor.transpose(tps[:, m, :], src[:, m, :], ident_bf[:])
                nc.scalar.copy(out=trig_t[:, j, :, :], in_=tps[:])
            return trig_t

        def c_tables(trig_t, t):
            banks = []
            for j in range(2):
                cps = psum.tile([P, 4, DH], F32, tag="cps", bufs=2, name="cps")
                for i in range(4):
                    nc.tensor.matmul(out=cps[:, i, :], lhsT=trig_t[:, 0, 4 * j + i, :], rhs=dmat[:, 2 + 2 * t, :],
                                     start=True, stop=False)
                    nc.tensor.matmul(out=cps[:, i, :], lhsT=trig_t[:, 1, 4 * j + i, :], rhs=dmat[:, 3 + 2 * t, :],
                                     start=False, stop=True)
                banks.append(cps)
            return banks

        def c_copy(banks, c_sb, j):
            nc.scalar.copy(out=c_sb[:, j, :], in_=banks[j][:, 1, :])

        def tab_k_pair(trig_t, m0):
            tps = psum.tile([P, 2, 4 * HALF], F32, tag="bank", bufs=6, name="tabps")
            for i in range(2):
                out4 = tps[:, i, :].rearrange("p (k e) -> p k e", k=4)
                for j, out_j in ((0, out4[:, 0:4:3, :]), (1, out4[:, 1:3, :])):
                    nc.tensor.matmul(out=out_j, lhsT=trig_t[:, j, m0 + i, :],
                                     rhs=unit2[:, j, :].rearrange("p (k e) -> p k e", k=2), start=True, stop=False)
                    nc.tensor.matmul(out=out_j, lhsT=trig_t[:, j, m0 + i, :],
                                     rhs=dmat[:, j, :].rearrange("p (k e) -> p k e", k=2), start=False, stop=True)
            nc.scalar.copy(out=tab_k[:, m0 : m0 + 2, :], in_=tps[:])

        tab_q = const.tile([P, MT, 4 * HALF], F32, name="tab_q")
        tab_k = const.tile([P, MT, 4 * HALF], F32, name="tab_k")
        c_q = const.tile([P, 2, DH], F32, name="c_q")
        c_k = const.tile([P, 2, DH], F32, name="c_k")


        operands = {}

        def operand(name, srcs):
            rows = 256 * len(srcs)
            operands[name] = {
                "srcs": srcs,
                "grouped": work.tile([P, 8 * rows], BF16, tag="grouped", bufs=2, name="grouped", align_bytes=64),
                "codes": const.tile([P, 2 * rows], U32, name="codes_" + name, align_bytes=64),
                "scales": const.tile([P, 2 * rows], U8, name="scales_" + name, align_bytes=64),
                "banks": [],
            }

        def keep_clock(out):
            nc.tensor.matmul(out=out, lhsT=zeros[:], rhs=zeros[:], start=True, stop=True)

        def turn(name, s, g):
            tp = psum.tile([P, 2, 256], F32, tag="bank", bufs=6, name="tp")
            if name in CLOCKED:
                keep_clock(tp[:, 0, 0:P])
            for c in range(2):
                if name == "q0":
                    words = w_first[g][:, 2 * s + c, :].bitcast(F32)
                else:
                    words = operands[name]["srcs"][s][:, c, 512 * g : 512 * (g + 1)].bitcast(F32)
                for u in range(2):
                    nc.tensor.transpose(tp[:, u, c * P : (c + 1) * P], words[:, u::2], ident[:])
            operands[name]["banks"].append((s, g, tp))

        def turn_x_tile(m):
            tp = psum.tile([P, 2, 2, P], F32, tag="bank", bufs=6, name="tp")
            for n in range(FIRST_CLOCK if m == 0 else SECOND_CLOCK):
                keep_clock(tp[:, 0, 0, :])
            words = x_first[m][:].bitcast(F32)
            for g in range(2):
                for u in range(2):
                    nc.tensor.transpose(tp[:, g, u, :], words[:, 256 * g + u : 256 * (g + 1) : 2], ident[:])
            return tp

        def finish_x_tile(m, tp):
            o = operands["x0"]
            gw = o["grouped"][:].bitcast(F32).rearrange("p (g r u) -> p g r u", g=2, u=2)
            nc.scalar.copy(out=gw[:, :, m * P : (m + 1) * P, :], in_=tp[:].rearrange("p g u r -> p g r u"))
            for g in range(2):
                c0 = 256 * g + m * P
                quantise("x0", c0, c0 + P)

        def copy_out(name, vector=False):
            s, g, tp = operands[name]["banks"].pop(0)
            rows = 256 * len(operands[name]["srcs"])
            w0 = (g * rows + s * 256) * 2
            gw = operands[name]["grouped"][:].bitcast(F32)
            eng = nc.vector.tensor_copy if vector else nc.scalar.copy
            eng(out=gw[:, w0 : w0 + 512].rearrange("p (r u) -> p r u", u=2), in_=tp[:].rearrange("p u r -> p r u"))

        def quantise(name, c0, c1):
            o = operands[name]
            nc.vector.quantize_mx(out=o["codes"][:, c0:c1].bitcast(E5X4), scales=o["scales"][:, c0:c1],
                                  in_=o["grouped"][:, 4 * c0 : 4 * c1])

        def mx_bank(m, key):
            acc = psum.tile([P, 512], F32, tag="bank", bufs=6, name="acc")
            pair, half = divmod(m, 2)
            xo, wo = operands["x%d" % pair], operands[key]
            for g in range(2):
                xcols = slice(g * 256 + half * P, g * 256 + (half + 1) * P)
                wcols = slice(g * 512, (g + 1) * 512)
                nc.tensor.matmul_mx(
                    out=acc[:],
                    lhsT=xo["codes"][:, xcols].bitcast(E5X4), lhsT_scale=xo["scales"][:, xcols],
                    rhs=wo["codes"][:, wcols].bitcast(E5X4), rhs_scale=wo["scales"][:, wcols],
                    start=(g == 0), stop=(g == 1),
                )
            return acc

        def out_view(out, h0):
            return out[0, h0 : h0 + 4, :, :].rearrange("h (p m) d -> p h m d", m=MT)

        CHUNKS = ["q0", "q1", "q2", "q3", "k"]
        N_BANKS = 8 * len(CHUNKS)
        bank = {}

        plan_turn = {0: [("x3", 0, 0), ("x3", 0, 1)], 1: [("q1", 0, 0), ("q1", 0, 1)], 2: [("q1", 1, 0), ("q1", 1, 1)]}
        plan_quant = {1: ["x2"], 3: ["x3"], 5: ["q1"]}
        for start, name in ((6, "q2"), (10, "v"), (14, "q3"), (18, "k")):
            for j in range(4):
                plan_turn[start + j] = [(name, j // 2, j % 2)]
            plan_quant[start + QLAG] = [name]
        v_steps = {V0 + VSTEP * j: j for j in range(8)}
        k_table_steps = {22: 0, 23: 2, 24: 4, 25: 6}
        c_copy_steps = {6: 0, 7: 1}

        def kind(i):
            if i in O_SET:
                return "O"
            return "V"

        def multiply(i):
            bank[i] = {"acc": mx_bank(i % 8, CHUNKS[i // 8])}

        def products(i):
            b = bank[i]
            tab = tab_k if i >= 32 else tab_q
            b["prod"] = work.tile([P, 4, 4 * HALF], F32, tag="prod", bufs=6, name="prod")
            nc.vector.tensor_tensor(
                out=b["prod"][:].rearrange("p h (k d) -> p h k d", k=2),
                in0=tab[:, i % 8, :].rearrange("p (k d) -> p k d", k=2).unsqueeze(1).to_broadcast([P, 4, 2, DH]),
                in1=b["acc"][:].rearrange("p (h d) -> p h d", h=4).unsqueeze(2).to_broadcast([P, 4, 2, DH]),
                op=ALU.mult,
            )

        def squares(i):
            b = bank[i]
            ss = work.tile([P, 4], F32, tag="ss", bufs=8, name="ss")
            junk = work.tile([P, 4, DH], F32, tag="junk", bufs=1, name="junk")
            for h in range(4):
                nc.scalar.activation(out=junk[:, h, :], in_=b["acc"][:, h * DH : (h + 1) * DH], func=ACT.Square,
                                     accum_out=ss[:, h : h + 1])
            b["rinv"] = work.tile([P, 4], F32, tag="rinv", bufs=8, name="rinv")
            nc.scalar.activation(out=b["rinv"][:], in_=ss[:], func=ACT.Abs_reciprocal_sqrt, bias=EPS, scale=1.0 / DH)

        def add_terms(i):
            b = bank[i]
            prod4 = b["prod"][:].rearrange("p h (k e) -> p h k e", k=4)
            b["rot"] = work.tile([P, 4, DH], F32, tag="rot", bufs=6, name="rot")
            adder = nc.vector if i == N_BANKS - 1 else nc.gpsimd
            adder.tensor_tensor(out=b["rot"][:].rearrange("p h (t e) -> p h t e", t=2),
                                in0=prod4[:, :, 0:4:3, :], in1=prod4[:, :, 1:3, :], op=ALU.add)

        def group(i):
            return 4 if i < 36 else 2 if i < 38 else 1

        pair_out = {}

        def out_tile(i):
            g = group(i)
            if i // g * g not in pair_out:
                pair_out[i // g * g] = [work.tile([P, 4, g, DH], F32, tag="o4" if g == 4 else "o", bufs=5 if g == 4 else 3, name="o"), 0]
            return pair_out[i // g * g][0]

        def store(i):
            g = group(i)
            i0 = i // g * g
            pair_out[i0][1] = pair_out[i0][1] + 1
            if pair_out[i0][1] == g:
                out, h0, m = (out_1, 0, i0 % 8) if i0 >= 32 else (out_0, 4 * (i0 // 8), i0 % 8)
                step = 2 if i == N_BANKS - 1 else 4
                for h in range(0, 4, step):
                    nc.sync.dma_start(out=out_view(out, h0)[:, h : h + step, m : m + g, :], in_=pair_out[i0][0][:, h : h + step, :, :])

        def last_vector(i):
            b, o = bank[i], out_tile(i)
            cps = c_banks["k" if i >= 32 else "q"][(i % 8) // 4]
            for h in range(4):
                nc.vector.scalar_tensor_tensor(out=o[:, h, i % group(i), :], in0=b["rot"][:, h, :], scalar=b["rinv"][:, h : h + 1],
                                               in1=cps[:, i % 4, :], op0=ALU.mult, op1=ALU.add)
            store(i)

        def scale_scalar(i):
            b = bank[i]
            b["scaled"] = work.tile([P, 4, DH], F32, tag="scaled", bufs=4, name="scaled")
            for h in range(4):
                nc.scalar.activation(out=b["scaled"][:, h, :], in_=b["rot"][:, h, :], func=ACT.Copy, scale=b["rinv"][:, h : h + 1])

        def shift_gpsimd(i):
            o = out_tile(i)
            c_sb = c_k if i >= 32 else c_q
            nc.gpsimd.tensor_tensor(out=o[:, :, i % group(i), :], in0=bank[i]["scaled"][:],
                                    in1=c_sb[:, i % 8 // 4, :].unsqueeze(1).to_broadcast([P, 4, DH]), op=ALU.add)
            store(i)

        v_tiles = {}

        def copy_v(m, acc):
            if m % 4 == 0:
                v_tiles["o"] = work.tile([P, 4, 4, DH], F32, tag="o4", bufs=5, name="ov")
            nc.scalar.copy(out=v_tiles["o"][:, :, m % 4, :], in_=acc[:].rearrange("p (h d) -> p h d", h=4))
            if m % 4 == 3:
                nc.sync.dma_start(out=out_view(out_2, 0)[:, :, m - 3 : m + 1, :], in_=v_tiles["o"][:])

        operand("x0", [None])
        operand("q0", [None, None])
        gain = const.tile([P, 2 * DH], F32, name="gain")
        with tc.manual_schedule(engines={mybir.EngineType.PE}):
            tp0 = turn_x_tile(0)
            finish_x_tile(0, tp0)
            turn("q0", 0, 0)
            turn("q0", 1, 0)
            spread = spread_vectors()
            turn("q0", 0, 1)
            turn("q0", 1, 1)
        nc.scalar.copy(out=gain[:], in_=spread[0][:, 0, :])
        for g in range(2):
            copy_out("q0")
            copy_out("q0", True)
            quantise("q0", 512 * g, 512 * (g + 1))
        for lo, hi in Q_TABLE_PARTS:
            q_table(gain[:], lo, hi)
        multiply(0)
        tp1 = turn_x_tile(1)
        finish_x_tile(1, tp1)
        multiply(1)
        operand("x1", [x_sb[1]])
        turn("x1", 0, 0)
        copy_out("x1")
        turn("x1", 0, 1)
        copy_out("x1")
        operand("x2", [x_sb[2]])
        turn("x2", 0, 0)
        turn("x2", 0, 1)
        quantise("x1", 0, 512)
        trig_t = trig_transposed()
        c_banks = {}
        late_constants(spread)
        c_banks["q"] = c_tables(trig_t, 0)
        pending_copy = ["x2", "x2"]
        pending_v = []
        for i in range(N_BANKS + 4):
            while pending_copy:
                copy_out(pending_copy.pop(0))
            if i < N_BANKS:
                products(i)
                squares(i)
                add_terms(i)
            if pending_v:
                copy_v(*pending_v.pop(0))
            for j in range(N_BANKS):
                if kind(j) == "V" and i == min(j + LAG_V, max(j, N_BANKS - 1)):
                    last_vector(j)
            for name in plan_quant.get(i, []):
                quantise(name, 0, 512 if name[0] == "x" else 1024)
            j = i - LAG_S
            if 0 <= j < N_BANKS and kind(j) != "V":
                scale_scalar(j)
            j = i - LAG_G
            if 0 <= j < N_BANKS and kind(j) != "V":
                shift_gpsimd(j)
            if i + AHEAD < N_BANKS:
                multiply(i + AHEAD)
            if i in v_steps:
                pending_v.append((v_steps[i], mx_bank(v_steps[i], "v")))
            for name, s, g in plan_turn.get(i, []):
                if name not in operands:
                    operand(name, [x_sb[int(name[1])]] if name[0] == "x" else w_sb[name])
                turn(name, s, g)
                pending_copy.append(name)
            if i == 3:
                load_w("q3", wq, 1536)
            if i == 4:
                load_w("k", wk, 0)
            if i in k_table_steps:
                tab_k_pair(trig_t, k_table_steps[i])
            if i == 31:
                c_banks["k"] = c_tables(trig_t, 1)
            if i in c_copy_steps:
                c_copy(c_banks["q"], c_q, c_copy_steps[i])
            if i == 32:
                c_copy(c_banks["k"], c_k, 0)
